import numpy as np
import ml_dtypes

BF16 = ml_dtypes.bfloat16


def bf(x):
    return np.asarray(x, np.float32).astype(BF16)


def f32(x):
    return np.asarray(x, np.float32)


def f64(x):
    return np.asarray(x).astype(np.float64)


def striped(idx):
    return np.tile(idx.reshape(-1, 16).T, (8, 1))


C, S, B, T, N = 128, 2048, 4, 64, 256
EPS = 1e-6


def pos_encoding(t, d):
    pos = np.arange(t, dtype=np.float32)[:, None]
    div = np.exp(np.arange(0, d, 2, dtype=np.float32) * np.float32(-np.log(10000.0) / d))
    ang = pos * div
    return np.stack([np.sin(ang), np.cos(ang)], axis=-1).reshape(t, d)


def setup_inputs():
    return {"emb": f32(np.random.standard_normal((C, S))), "pe": f32(np.ascontiguousarray(pos_encoding(T, C).T)), "w1": bf(2.0 * np.random.standard_normal((C, C)) / np.sqrt(C)), "b1": f32(0.1 * np.random.standard_normal((C, 1))), "w2": bf(2.0 * np.random.standard_normal((C, C)) / np.sqrt(C)), "b2": f32(0.1 * np.random.standard_normal((C, 1))), "gamma": f32(1.0 + 0.1 * np.random.standard_normal((C, 1))), "beta": f32(0.1 * np.random.standard_normal((C, 1))), "offs": striped(np.random.permutation(np.tile(np.arange(S), 2))[:N])}


def reference(emb, pe, w1, b1, w2, b2, gamma, beta, offs):
    idx = offs[:16].T.reshape(-1)
    x = f64(emb)[:, idx]
    a = f64(pe)
    e = np.exp(a[:, :, None] * a[:, None, :])
    p = e / e.sum(axis=2, keepdims=True)
    v = np.einsum("cit,cbt->cbi", p, x.reshape(C, B, T)).reshape(C, N)
    h = np.maximum(f64(w1).T @ v + f64(b1), 0.0)
    r = np.maximum(f64(w2).T @ h + f64(b2), 0.0)
    mean = r.mean(axis=0, keepdims=True)
    std = np.sqrt(((r - mean) ** 2).sum(axis=0, keepdims=True) / (C - 1))
    return x + (f64(gamma) * (r - mean) / (std + EPS) + f64(beta))

@@ -1,0 +1,138 @@
+import concourse.mybir as mybir
+
+F32 = mybir.dt.float32
+BF16 = mybir.dt.bfloat16
+U16 = mybir.dt.uint16
+ALU = mybir.AluOpType
+ACT = mybir.ActivationFunctionType
+AXIS = mybir.AxisListType
+
+C = 128
+S = 2048
+B = 4
+T = 64
+N = B * T
+EPS = 1e-6
+TINY = 1e-30
+CHUNK = 16
+
+FLOPS = 2 * C * N * T + 2 * 2 * C * C * N
+BYTES = 4 * C * N + 4 * C * T + 2 * 2 * C * C + 4 * 4 * C + 2 * C * (N // 16) + 4 * C * N
+
+
+def tile_pamcharecoder_kernel(tc, emb, pe, w1, b1, w2, b2, gamma, beta, offs, out):
+    nc = tc.nc
+    with (
+        tc.tile_pool(name="held", bufs=1) as held,
+        tc.psum_pool(name="psum", bufs=1) as psum,
+    ):
+        offsets = held.tile([C, N // 16], U16, name="offsets")
+        nc.sync.dma_start(offsets[:], offs)
+        code = held.tile([C, T], F32, name="code")
+        nc.scalar.dma_start(code[:], pe)
+        table = held.tile([C, S], F32, name="table")
+        nc.sync.dma_start(table[:], emb)
+        w1_sb = held.tile([C, C], BF16, name="w1_sb")
+        nc.gpsimd.dma_start(w1_sb[:], w1)
+        w2_sb = held.tile([C, C], BF16, name="w2_sb")
+        nc.gpsimd.dma_start(w2_sb[:], w2)
+        b1_sb = held.tile([C, 1], F32, name="b1_sb")
+        nc.gpsimd.dma_start(b1_sb[:], b1)
+        b2_sb = held.tile([C, 1], F32, name="b2_sb")
+        nc.gpsimd.dma_start(b2_sb[:], b2)
+        gamma_sb = held.tile([C, 1], F32, name="gamma_sb")
+        nc.gpsimd.dma_start(gamma_sb[:], gamma)
+        beta_sb = held.tile([C, 1], F32, name="beta_sb")
+        nc.gpsimd.dma_start(beta_sb[:], beta)
+
+        ones = held.tile([C, C], F32, name="ones")
+        nc.gpsimd.memset(ones[:], 1.0)
+        tiny = held.tile([C, 1], F32, name="tiny")
+        nc.gpsimd.memset(tiny[:], TINY)
+
+        neg_max = held.tile([C, 1], F32, name="neg_max")
+        nc.vector.tensor_reduce(neg_max[:], code[:], axis=AXIS.X, op=ALU.max, negate=True)
+        neg_min = held.tile([C, 1], F32, name="neg_min")
+        nc.vector.tensor_reduce(neg_min[:], code[:], axis=AXIS.X, op=ALU.min, negate=True)
+        by_max = held.tile([C, T], F32, name="by_max")
+        nc.vector.tensor_scalar_mul(by_max[:], code[:], neg_max[:, 0:1])
+        shift = held.tile([C, T], F32, name="shift")
+        nc.vector.scalar_tensor_tensor(
+            shift[:], code[:], neg_min[:, 0:1], by_max[:], op0=ALU.mult, op1=ALU.min
+        )
+
+        weights = held.tile([C, T, B, T], F32, name="weights")
+        row_sum = held.tile([C, T], F32, name="row_sum")
+        for i in range(T):
+            nc.scalar.activation(
+                weights[:, i, :, :],
+                code[:].unsqueeze(1).to_broadcast([C, B, T]),
+                ACT.Exp,
+                bias=shift[:, i : i + 1],
+                scale=code[:, i : i + 1],
+                accum_out=row_sum[:, i : i + 1],
+            )
+        inv_sum = held.tile([C, T], F32, name="inv_sum")
+        nc.vector.reciprocal(inv_sum[:], row_sum[:])
+
+        prod = held.tile([C, T, N], F32, name="prod")
+        mixed = held.tile([C, B, T], F32, name="mixed")
+        for first in range(0, T, CHUNK):
+            for i in range(first, first + CHUNK):
+                nc.vector.tensor_tensor(
+                    prod[:, i, :],
+                    table[:].indirect(offsets[:]),
+                    weights[:, i, :, :].rearrange("c u t -> c (u t)"),
+                    ALU.mult,
+                )
+            nc.vector.tensor_reduce(
+                mixed[:, :, first : first + CHUNK],
+                prod[:, first : first + CHUNK, :].rearrange("c i (u t) -> c u i t", u=B),
+                axis=AXIS.X,
+                op=ALU.add,
+            )
+        v_bf = held.tile([C, B, T], BF16, name="v_bf")
+        nc.vector.scalar_tensor_tensor(
+            v_bf[:],
+            mixed[:],
+            float(B),
+            inv_sum[:].unsqueeze(1).to_broadcast([C, B, T]),
+            op0=ALU.mult,
+            op1=ALU.mult,
+        )
+
+        h_ps = psum.tile([C, N], F32, name="h_ps")
+        nc.tensor.matmul(h_ps[:], w1_sb[:], v_bf[:].rearrange("c u i -> c (u i)"), start=True, stop=True)
+        h_bf = held.tile([C, N], BF16, name="h_bf")
+        nc.scalar.activation(h_bf[:], h_ps[:], ACT.Relu, bias=b1_sb[:, 0:1])
+        r_ps = psum.tile([C, N], F32, name="r_ps")
+        nc.tensor.matmul(r_ps[:], w2_sb[:], h_bf[:], start=True, stop=True)
+        r_sb = held.tile([C, N], F32, name="r_sb")
+        nc.scalar.activation(r_sb[:], r_ps[:], ACT.Relu, bias=b2_sb[:, 0:1])
+
+        sum_ps = psum.tile([C, N], F32, name="sum_ps")
+        nc.tensor.matmul(sum_ps[:], ones[:], r_sb[:], start=True, stop=True)
+        centred = held.tile([C, N], F32, name="centred")
+        nc.vector.scalar_tensor_tensor(
+            centred[:], sum_ps[:], -1.0 / C, r_sb[:], op0=ALU.mult, op1=ALU.add
+        )
+        squared = held.tile([C, N], F32, name="squared")
+        nc.scalar.activation(squared[:], centred[:], ACT.Square)
+        ssq_ps = psum.tile([C, N], F32, name="ssq_ps")
+        nc.tensor.matmul(ssq_ps[:], ones[:], squared[:], start=True, stop=True)
+        std = held.tile([C, N], F32, name="std")
+        nc.scalar.activation(std[:], ssq_ps[:], ACT.Sqrt, bias=tiny[:, 0:1], scale=1.0 / (C - 1))
+        std_eps = held.tile([C, N], F32, name="std_eps")
+        nc.vector.tensor_scalar_add(std_eps[:], std[:], EPS)
+        inv_std = held.tile([C, N], F32, name="inv_std")
+        nc.vector.reciprocal(inv_std[:], std_eps[:])
+        normed = held.tile([C, N], F32, name="normed")
+        nc.vector.tensor_tensor(normed[:], centred[:], inv_std[:], ALU.mult)
+        scaled = held.tile([C, N], F32, name="scaled")
+        nc.vector.tensor_scalar(
+            scaled[:], normed[:], gamma_sb[:, 0:1], beta_sb[:, 0:1], op0=ALU.mult, op1=ALU.add
+        )
+
+        result = held.tile([C, N], F32, name="result")
+        nc.vector.tensor_tensor(result[:], table[:].indirect(offsets[:]), scaled[:], ALU.add)
+        nc.sync.dma_start(out, result[:])

@@ -1,4 +1,5 @@
 import concourse.mybir as mybir
+from concourse.masks import make_identity
 
 F32 = mybir.dt.float32
 BF16 = mybir.dt.bfloat16
@@ -14,7 +15,13 @@ T = 64
 N = B * T
 EPS = 1e-6
 TINY = 1e-30
+SKEW = B - 1
+ROWS = T + SKEW
 CHUNK = 16
+CHUNKS = T // CHUNK
+COLS = B * CHUNK
+STAGES = 5
+SPACING = 2
 
 FLOPS = 2 * C * N * T + 2 * 2 * C * C * N
 BYTES = 4 * C * N + 4 * C * T + 2 * 2 * C * C + 4 * 4 * C + 2 * C * (N // 16) + 4 * C * N
@@ -45,6 +52,9 @@ def tile_pamcharecoder_kernel(tc, emb, pe, w1, b1, w2, b2, gamma, beta, offs, ou
         beta_sb = held.tile([C, 1], F32, name="beta_sb")
         nc.gpsimd.dma_start(beta_sb[:], beta)
 
+        centre = held.tile([C, C], F32, name="centre")
+        make_identity(nc, centre[:])
+        nc.gpsimd.tensor_scalar_add(centre[:], centre[:], -1.0 / C)
         ones = held.tile([C, C], F32, name="ones")
         nc.gpsimd.memset(ones[:], 1.0)
         tiny = held.tile([C, 1], F32, name="tiny")
@@ -61,78 +71,95 @@ def tile_pamcharecoder_kernel(tc, emb, pe, w1, b1, w2, b2, gamma, beta, offs, ou
             shift[:], code[:], neg_min[:, 0:1], by_max[:], op0=ALU.mult, op1=ALU.min
         )
 
-        weights = held.tile([C, T, B, T], F32, name="weights")
-        row_sum = held.tile([C, T], F32, name="row_sum")
-        for i in range(T):
-            nc.scalar.activation(
-                weights[:, i, :, :],
-                code[:].unsqueeze(1).to_broadcast([C, B, T]),
-                ACT.Exp,
-                bias=shift[:, i : i + 1],
-                scale=code[:, i : i + 1],
-                accum_out=row_sum[:, i : i + 1],
-            )
-        inv_sum = held.tile([C, T], F32, name="inv_sum")
-        nc.vector.reciprocal(inv_sum[:], row_sum[:])
-
-        prod = held.tile([C, T, N], F32, name="prod")
-        mixed = held.tile([C, B, T], F32, name="mixed")
-        for first in range(0, T, CHUNK):
-            for i in range(first, first + CHUNK):
-                nc.vector.tensor_tensor(
-                    prod[:, i, :],
-                    table[:].indirect(offsets[:]),
-                    weights[:, i, :, :].rearrange("c u t -> c (u t)"),
-                    ALU.mult,
+        weights = held.tile([C, ROWS, T], F32, name="weights")
+        row_sum = held.tile([C, ROWS], F32, name="row_sum")
+        inv_sum = held.tile([C, ROWS], F32, name="inv_sum")
+        for first in range(0, ROWS, CHUNK):
+            last = min(first + CHUNK, ROWS)
+            for e in range(first, last):
+                i = (e - SKEW) % T
+                nc.scalar.activation(
+                    weights[:, e, :],
+                    code[:],
+                    ACT.Exp,
+                    bias=shift[:, i : i + 1],
+                    scale=code[:, i : i + 1],
+                    accum_out=row_sum[:, e : e + 1],
                 )
-            nc.vector.tensor_reduce(
-                mixed[:, :, first : first + CHUNK],
-                prod[:, first : first + CHUNK, :].rearrange("c i (u t) -> c u i t", u=B),
-                axis=AXIS.X,
-                op=ALU.add,
-            )
-        v_bf = held.tile([C, B, T], BF16, name="v_bf")
-        nc.vector.scalar_tensor_tensor(
-            v_bf[:],
-            mixed[:],
-            float(B),
-            inv_sum[:].unsqueeze(1).to_broadcast([C, B, T]),
-            op0=ALU.mult,
-            op1=ALU.mult,
-        )
+            nc.vector.reciprocal(inv_sum[:, first:last], row_sum[:, first:last])
 
+        prod = held.tile([C, T, B, T], F32, name="prod")
+        v_bf = held.tile([C, N], BF16, name="v_bf")
         h_ps = psum.tile([C, N], F32, name="h_ps")
-        nc.tensor.matmul(h_ps[:], w1_sb[:], v_bf[:].rearrange("c u i -> c (u i)"), start=True, stop=True)
         h_bf = held.tile([C, N], BF16, name="h_bf")
-        nc.scalar.activation(h_bf[:], h_ps[:], ACT.Relu, bias=b1_sb[:, 0:1])
         r_ps = psum.tile([C, N], F32, name="r_ps")
-        nc.tensor.matmul(r_ps[:], w2_sb[:], h_bf[:], start=True, stop=True)
         r_sb = held.tile([C, N], F32, name="r_sb")
-        nc.scalar.activation(r_sb[:], r_ps[:], ACT.Relu, bias=b2_sb[:, 0:1])
-
-        sum_ps = psum.tile([C, N], F32, name="sum_ps")
-        nc.tensor.matmul(sum_ps[:], ones[:], r_sb[:], start=True, stop=True)
-        centred = held.tile([C, N], F32, name="centred")
-        nc.vector.scalar_tensor_tensor(
-            centred[:], sum_ps[:], -1.0 / C, r_sb[:], op0=ALU.mult, op1=ALU.add
-        )
+        d_ps = [psum.tile([C, COLS], F32, name=f"d_ps{chunk}") for chunk in range(CHUNKS)]
         squared = held.tile([C, N], F32, name="squared")
-        nc.scalar.activation(squared[:], centred[:], ACT.Square)
         ssq_ps = psum.tile([C, N], F32, name="ssq_ps")
-        nc.tensor.matmul(ssq_ps[:], ones[:], squared[:], start=True, stop=True)
         std = held.tile([C, N], F32, name="std")
-        nc.scalar.activation(std[:], ssq_ps[:], ACT.Sqrt, bias=tiny[:, 0:1], scale=1.0 / (C - 1))
-        std_eps = held.tile([C, N], F32, name="std_eps")
-        nc.vector.tensor_scalar_add(std_eps[:], std[:], EPS)
         inv_std = held.tile([C, N], F32, name="inv_std")
-        nc.vector.reciprocal(inv_std[:], std_eps[:])
         normed = held.tile([C, N], F32, name="normed")
-        nc.vector.tensor_tensor(normed[:], centred[:], inv_std[:], ALU.mult)
-        scaled = held.tile([C, N], F32, name="scaled")
-        nc.vector.tensor_scalar(
-            scaled[:], normed[:], gamma_sb[:, 0:1], beta_sb[:, 0:1], op0=ALU.mult, op1=ALU.add
-        )
+        scaled = held.tile([C, B, T], F32, name="scaled")
+
+        def finish(chunk, stage):
+            cols = slice(chunk * COLS, (chunk + 1) * COLS)
+            if stage == 0:
+                nc.tensor.matmul(h_ps[:, cols], w1_sb[:], v_bf[:, cols], start=True, stop=True)
+            elif stage == 1:
+                nc.scalar.activation(h_bf[:, cols], h_ps[:, cols], ACT.Relu, bias=b1_sb[:, 0:1])
+                nc.tensor.matmul(r_ps[:, cols], w2_sb[:], h_bf[:, cols], start=True, stop=True)
+            elif stage == 2:
+                nc.scalar.activation(r_sb[:, cols], r_ps[:, cols], ACT.Relu, bias=b2_sb[:, 0:1])
+                nc.tensor.matmul(d_ps[chunk][:], centre[:], r_sb[:, cols], start=True, stop=True)
+            elif stage == 3:
+                nc.scalar.activation(squared[:, cols], d_ps[chunk][:], ACT.Square)
+                nc.tensor.matmul(ssq_ps[:, cols], ones[:], squared[:, cols], start=True, stop=True)
+            elif stage == 4:
+                nc.scalar.activation(
+                    std[:, cols], ssq_ps[:, cols], ACT.Sqrt, bias=tiny[:, 0:1], scale=1.0 / (C - 1)
+                )
+                nc.vector.tensor_scalar_add(std[:, cols], std[:, cols], EPS)
+                nc.vector.reciprocal(inv_std[:, cols], std[:, cols])
+                nc.vector.tensor_tensor(normed[:, cols], d_ps[chunk][:], inv_std[:, cols], ALU.mult)
+                nc.vector.tensor_scalar(
+                    scaled[:, :, chunk * CHUNK : (chunk + 1) * CHUNK],
+                    normed[:, cols].rearrange("c (u i) -> c u i", u=B),
+                    gamma_sb[:, 0:1],
+                    beta_sb[:, 0:1],
+                    op0=ALU.mult,
+                    op1=ALU.add,
+                )
+
+        for step in range(T):
+            nc.vector.tensor_tensor(
+                prod[:, step, :, :].rearrange("c u t -> c (u t)"),
+                table[:].indirect(offsets[:]),
+                weights[:, step : step + B, :].rearrange("c e t -> c (e t)"),
+                ALU.mult,
+            )
+            for u in range(B):
+                chunk, within = divmod((step + u - SKEW) % T, CHUNK)
+                column = chunk * COLS + u * CHUNK + within
+                with nc.allow_low_precision(reason="v is rounded once to bfloat16"):
+                    nc.scalar.activation(
+                        prod[:, step, u, :],
+                        prod[:, step, u, :],
+                        ACT.Copy,
+                        scale=inv_sum[:, step + u : step + u + 1],
+                        accum_out=v_bf[:, column : column + 1],
+                    )
+            chunk, since = divmod(step - (CHUNK + SKEW - 1), CHUNK)
+            if chunk >= 0 and since % SPACING == 0 and since // SPACING < STAGES:
+                finish(chunk, since // SPACING)
+        for stage in range(STAGES):
+            finish(CHUNKS - 1, stage)
 
         result = held.tile([C, N], F32, name="result")
-        nc.vector.tensor_tensor(result[:], table[:].indirect(offsets[:]), scaled[:], ALU.add)
+        nc.vector.tensor_tensor(
+            result[:],
+            table[:].indirect(offsets[:]),
+            scaled[:].rearrange("c u i -> c (u i)"),
+            ALU.add,
+        )
         nc.sync.dma_start(out, result[:])

@@ -22,6 +22,7 @@ CHUNKS = T // CHUNK
 COLS = B * CHUNK
 STAGES = 5
 SPACING = 2
+BATCH = 8
 
 FLOPS = 2 * C * N * T + 2 * 2 * C * C * N
 BYTES = 4 * C * N + 4 * C * T + 2 * 2 * C * C + 4 * 4 * C + 2 * C * (N // 16) + 4 * C * N
@@ -84,12 +85,15 @@ def tile_pamcharecoder_kernel(tc, emb, pe, w1, b1, w2, b2, gamma, beta, offs, ou
                     ACT.Exp,
                     bias=shift[:, i : i + 1],
                     scale=code[:, i : i + 1],
-                    accum_out=row_sum[:, e : e + 1],
                 )
+            nc.vector.tensor_reduce(
+                row_sum[:, first:last], weights[:, first:last, :], axis=AXIS.X, op=ALU.add
+            )
             nc.vector.reciprocal(inv_sum[:, first:last], row_sum[:, first:last])
 
         prod = held.tile([C, T, B, T], F32, name="prod")
         v_bf = held.tile([C, N], BF16, name="v_bf")
+        last_sums = held.tile([C, T], F32, name="last_sums")
         h_ps = psum.tile([C, N], F32, name="h_ps")
         h_bf = held.tile([C, N], BF16, name="h_bf")
         r_ps = psum.tile([C, N], F32, name="r_ps")
@@ -105,6 +109,12 @@ def tile_pamcharecoder_kernel(tc, emb, pe, w1, b1, w2, b2, gamma, beta, offs, ou
         def finish(chunk, stage):
             cols = slice(chunk * COLS, (chunk + 1) * COLS)
             if stage == 0:
+                nc.gpsimd.tensor_tensor(
+                    v_bf[:, (chunk + 1) * COLS - CHUNK : (chunk + 1) * COLS],
+                    last_sums[:, chunk * CHUNK : (chunk + 1) * CHUNK],
+                    inv_sum[:, SKEW + chunk * CHUNK : SKEW + (chunk + 1) * CHUNK],
+                    ALU.mult,
+                )
                 nc.tensor.matmul(h_ps[:, cols], w1_sb[:], v_bf[:, cols], start=True, stop=True)
             elif stage == 1:
                 nc.scalar.activation(h_bf[:, cols], h_ps[:, cols], ACT.Relu, bias=b1_sb[:, 0:1])
@@ -138,7 +148,7 @@ def tile_pamcharecoder_kernel(tc, emb, pe, w1, b1, w2, b2, gamma, beta, offs, ou
                 weights[:, step : step + B, :].rearrange("c e t -> c (e t)"),
                 ALU.mult,
             )
-            for u in range(B):
+            for u in range(B - 1):
                 chunk, within = divmod((step + u - SKEW) % T, CHUNK)
                 column = chunk * COLS + u * CHUNK + within
                 with nc.allow_low_precision(reason="v is rounded once to bfloat16"):
@@ -149,6 +159,13 @@ def tile_pamcharecoder_kernel(tc, emb, pe, w1, b1, w2, b2, gamma, beta, offs, ou
                         scale=inv_sum[:, step + u : step + u + 1],
                         accum_out=v_bf[:, column : column + 1],
                     )
+            if (step + 1) % BATCH == 0:
+                nc.vector.tensor_reduce(
+                    last_sums[:, step + 1 - BATCH : step + 1],
+                    prod[:, step + 1 - BATCH : step + 1, B - 1, :],
+                    axis=AXIS.X,
+                    op=ALU.add,
+                )
             chunk, since = divmod(step - (CHUNK + SKEW - 1), CHUNK)
             if chunk >= 0 and since % SPACING == 0 and since // SPACING < STAGES:
                 finish(chunk, since // SPACING)

@@ -22,6 +22,7 @@ CHUNKS = T // CHUNK
 COLS = B * CHUNK
 STAGES = 5
 SPACING = 2
+AHEAD = 4
 BATCH = 8
 
 FLOPS = 2 * C * N * T + 2 * 2 * C * C * N
@@ -75,23 +76,25 @@ def tile_pamcharecoder_kernel(tc, emb, pe, w1, b1, w2, b2, gamma, beta, offs, ou
         weights = held.tile([C, ROWS, T], F32, name="weights")
         row_sum = held.tile([C, ROWS], F32, name="row_sum")
         inv_sum = held.tile([C, ROWS], F32, name="inv_sum")
-        for first in range(0, ROWS, CHUNK):
-            last = min(first + CHUNK, ROWS)
-            for e in range(first, last):
-                i = (e - SKEW) % T
-                nc.scalar.activation(
-                    weights[:, e, :],
-                    code[:],
-                    ACT.Exp,
-                    bias=shift[:, i : i + 1],
-                    scale=code[:, i : i + 1],
-                )
-            nc.vector.tensor_reduce(
-                row_sum[:, first:last], weights[:, first:last, :], axis=AXIS.X, op=ALU.add
+        for e in range(ROWS):
+            i = (e - SKEW) % T
+            nc.scalar.activation(
+                weights[:, e, :],
+                code[:],
+                ACT.Exp,
+                bias=shift[:, i : i + 1],
+                scale=code[:, i : i + 1],
             )
-            nc.vector.reciprocal(inv_sum[:, first:last], row_sum[:, first:last])
+
+        def sum_rows(group):
+            rows = slice(group * CHUNK, min((group + 1) * CHUNK, ROWS))
+            nc.vector.tensor_reduce(row_sum[:, rows], weights[:, rows, :], axis=AXIS.X, op=ALU.add)
+            nc.vector.reciprocal(inv_sum[:, rows], row_sum[:, rows])
+
+        sum_rows(0)
 
         prod = held.tile([C, T, B, T], F32, name="prod")
+        unread = held.tile([C, T, B - 1, T], BF16, name="unread")
         v_bf = held.tile([C, N], BF16, name="v_bf")
         last_sums = held.tile([C, T], F32, name="last_sums")
         h_ps = psum.tile([C, N], F32, name="h_ps")
@@ -109,7 +112,7 @@ def tile_pamcharecoder_kernel(tc, emb, pe, w1, b1, w2, b2, gamma, beta, offs, ou
         def finish(chunk, stage):
             cols = slice(chunk * COLS, (chunk + 1) * COLS)
             if stage == 0:
-                nc.gpsimd.tensor_tensor(
+                nc.vector.tensor_tensor(
                     v_bf[:, (chunk + 1) * COLS - CHUNK : (chunk + 1) * COLS],
                     last_sums[:, chunk * CHUNK : (chunk + 1) * CHUNK],
                     inv_sum[:, SKEW + chunk * CHUNK : SKEW + (chunk + 1) * CHUNK],
@@ -153,12 +156,14 @@ def tile_pamcharecoder_kernel(tc, emb, pe, w1, b1, w2, b2, gamma, beta, offs, ou
                 column = chunk * COLS + u * CHUNK + within
                 with nc.allow_low_precision(reason="v is rounded once to bfloat16"):
                     nc.scalar.activation(
-                        prod[:, step, u, :],
+                        unread[:, step, u, :],
                         prod[:, step, u, :],
                         ACT.Copy,
                         scale=inv_sum[:, step + u : step + u + 1],
                         accum_out=v_bf[:, column : column + 1],
                     )
+            if step % CHUNK == AHEAD:
+                sum_rows(step // CHUNK + 1)
             if (step + 1) % BATCH == 0:
                 nc.vector.tensor_reduce(
                     last_sums[:, step + 1 - BATCH : step + 1],

@@ -22,7 +22,8 @@ CHUNKS = T // CHUNK
 COLS = B * CHUNK
 STAGES = 5
 SPACING = 2
-AHEAD = 4
+VECTOR_ROWS = 2 * CHUNK
+AHEAD = 12
 BATCH = 8
 
 FLOPS = 2 * C * N * T + 2 * 2 * C * C * N
@@ -84,14 +85,12 @@ def tile_pamcharecoder_kernel(tc, emb, pe, w1, b1, w2, b2, gamma, beta, offs, ou
                 ACT.Exp,
                 bias=shift[:, i : i + 1],
                 scale=code[:, i : i + 1],
+                accum_out=row_sum[:, e : e + 1] if e >= VECTOR_ROWS else None,
             )
-
-        def sum_rows(group):
-            rows = slice(group * CHUNK, min((group + 1) * CHUNK, ROWS))
+        for first in range(0, VECTOR_ROWS, CHUNK):
+            rows = slice(first, first + CHUNK)
             nc.vector.tensor_reduce(row_sum[:, rows], weights[:, rows, :], axis=AXIS.X, op=ALU.add)
             nc.vector.reciprocal(inv_sum[:, rows], row_sum[:, rows])
-
-        sum_rows(0)
 
         prod = held.tile([C, T, B, T], F32, name="prod")
         unread = held.tile([C, T, B - 1, T], BF16, name="unread")
@@ -162,8 +161,8 @@ def tile_pamcharecoder_kernel(tc, emb, pe, w1, b1, w2, b2, gamma, beta, offs, ou
                         scale=inv_sum[:, step + u : step + u + 1],
                         accum_out=v_bf[:, column : column + 1],
                     )
-            if step % CHUNK == AHEAD:
-                sum_rows(step // CHUNK + 1)
+            if step == AHEAD:
+                nc.vector.reciprocal(inv_sum[:, VECTOR_ROWS:], row_sum[:, VECTOR_ROWS:])
             if (step + 1) % BATCH == 0:
                 nc.vector.tensor_reduce(
                     last_sums[:, step + 1 - BATCH : step + 1],

@@ -131,17 +131,20 @@ def tile_pamcharecoder_kernel(tc, emb, pe, w1, b1, w2, b2, gamma, beta, offs, ou
                 nc.scalar.activation(
                     std[:, cols], ssq_ps[:, cols], ACT.Sqrt, bias=tiny[:, 0:1], scale=1.0 / (C - 1)
                 )
-                nc.vector.tensor_scalar_add(std[:, cols], std[:, cols], EPS)
-                nc.vector.reciprocal(inv_std[:, cols], std[:, cols])
-                nc.vector.tensor_tensor(normed[:, cols], d_ps[chunk][:], inv_std[:, cols], ALU.mult)
-                nc.vector.tensor_scalar(
-                    scaled[:, :, chunk * CHUNK : (chunk + 1) * CHUNK],
-                    normed[:, cols].rearrange("c (u i) -> c u i", u=B),
-                    gamma_sb[:, 0:1],
-                    beta_sb[:, 0:1],
-                    op0=ALU.mult,
-                    op1=ALU.add,
-                )
+
+        def apply_norm(chunk):
+            cols = slice(chunk * COLS, (chunk + 1) * COLS)
+            nc.vector.tensor_scalar_add(std[:, cols], std[:, cols], EPS)
+            nc.vector.reciprocal(inv_std[:, cols], std[:, cols])
+            nc.vector.tensor_tensor(normed[:, cols], d_ps[chunk][:], inv_std[:, cols], ALU.mult)
+            nc.vector.tensor_scalar(
+                scaled[:, :, chunk * CHUNK : (chunk + 1) * CHUNK],
+                normed[:, cols].rearrange("c (u i) -> c u i", u=B),
+                gamma_sb[:, 0:1],
+                beta_sb[:, 0:1],
+                op0=ALU.mult,
+                op1=ALU.add,
+            )
 
         for step in range(T):
             nc.vector.tensor_tensor(
@@ -173,8 +176,12 @@ def tile_pamcharecoder_kernel(tc, emb, pe, w1, b1, w2, b2, gamma, beta, offs, ou
             chunk, since = divmod(step - (CHUNK + SKEW - 1), CHUNK)
             if chunk >= 0 and since % SPACING == 0 and since // SPACING < STAGES:
                 finish(chunk, since // SPACING)
-        for stage in range(STAGES):
+        finish(CHUNKS - 1, 0)
+        for chunk in range(CHUNKS - 1):
+            apply_norm(chunk)
+        for stage in range(1, STAGES):
             finish(CHUNKS - 1, stage)
+        apply_norm(CHUNKS - 1)
 
         result = held.tile([C, N], F32, name="result")
         nc.vector.tensor_tensor(

@@ -22,7 +22,7 @@ CHUNKS = T // CHUNK
 COLS = B * CHUNK
 STAGES = 5
 SPACING = 2
-VECTOR_ROWS = 2 * CHUNK
+VECTOR_ROWS = CHUNK
 AHEAD = 12
 BATCH = 8
 

@@ -43,17 +43,17 @@ def tile_pamcharecoder_kernel(tc, emb, pe, w1, b1, w2, b2, gamma, beta, offs, ou
         table = held.tile([C, S], F32, name="table")
         nc.sync.dma_start(table[:], emb)
         w1_sb = held.tile([C, C], BF16, name="w1_sb")
-        nc.gpsimd.dma_start(w1_sb[:], w1)
+        nc.sync.dma_start(w1_sb[:], w1)
         w2_sb = held.tile([C, C], BF16, name="w2_sb")
-        nc.gpsimd.dma_start(w2_sb[:], w2)
+        nc.sync.dma_start(w2_sb[:], w2)
         b1_sb = held.tile([C, 1], F32, name="b1_sb")
-        nc.gpsimd.dma_start(b1_sb[:], b1)
+        nc.sync.dma_start(b1_sb[:], b1)
         b2_sb = held.tile([C, 1], F32, name="b2_sb")
-        nc.gpsimd.dma_start(b2_sb[:], b2)
+        nc.sync.dma_start(b2_sb[:], b2)
         gamma_sb = held.tile([C, 1], F32, name="gamma_sb")
-        nc.gpsimd.dma_start(gamma_sb[:], gamma)
+        nc.sync.dma_start(gamma_sb[:], gamma)
         beta_sb = held.tile([C, 1], F32, name="beta_sb")
-        nc.gpsimd.dma_start(beta_sb[:], beta)
+        nc.sync.dma_start(beta_sb[:], beta)
 
         centre = held.tile([C, C], F32, name="centre")
         make_identity(nc, centre[:])

@@ -25,6 +25,7 @@ SPACING = 2
 VECTOR_ROWS = CHUNK
 AHEAD = 12
 BATCH = 8
+SCALAR_CHUNKS = 2
 
 FLOPS = 2 * C * N * T + 2 * 2 * C * C * N
 BYTES = 4 * C * N + 4 * C * T + 2 * 2 * C * C + 4 * 4 * C + 2 * C * (N // 16) + 4 * C * N
@@ -93,7 +94,7 @@ def tile_pamcharecoder_kernel(tc, emb, pe, w1, b1, w2, b2, gamma, beta, offs, ou
             nc.vector.reciprocal(inv_sum[:, rows], row_sum[:, rows])
 
         prod = held.tile([C, T, B, T], F32, name="prod")
-        unread = held.tile([C, T, B - 1, T], BF16, name="unread")
+        unread = held.tile([C, T, B, T], BF16, name="unread")
         v_bf = held.tile([C, N], BF16, name="v_bf")
         last_sums = held.tile([C, T], F32, name="last_sums")
         h_ps = psum.tile([C, N], F32, name="h_ps")
@@ -111,12 +112,13 @@ def tile_pamcharecoder_kernel(tc, emb, pe, w1, b1, w2, b2, gamma, beta, offs, ou
         def finish(chunk, stage):
             cols = slice(chunk * COLS, (chunk + 1) * COLS)
             if stage == 0:
-                nc.vector.tensor_tensor(
-                    v_bf[:, (chunk + 1) * COLS - CHUNK : (chunk + 1) * COLS],
-                    last_sums[:, chunk * CHUNK : (chunk + 1) * CHUNK],
-                    inv_sum[:, SKEW + chunk * CHUNK : SKEW + (chunk + 1) * CHUNK],
-                    ALU.mult,
-                )
+                if chunk >= SCALAR_CHUNKS:
+                    nc.vector.tensor_tensor(
+                        v_bf[:, (chunk + 1) * COLS - CHUNK : (chunk + 1) * COLS],
+                        last_sums[:, chunk * CHUNK : (chunk + 1) * CHUNK],
+                        inv_sum[:, SKEW + chunk * CHUNK : SKEW + (chunk + 1) * CHUNK],
+                        ALU.mult,
+                    )
                 nc.tensor.matmul(h_ps[:, cols], w1_sb[:], v_bf[:, cols], start=True, stop=True)
             elif stage == 1:
                 nc.scalar.activation(h_bf[:, cols], h_ps[:, cols], ACT.Relu, bias=b1_sb[:, 0:1])
@@ -153,8 +155,10 @@ def tile_pamcharecoder_kernel(tc, emb, pe, w1, b1, w2, b2, gamma, beta, offs, ou
                 weights[:, step : step + B, :].rearrange("c e t -> c (e t)"),
                 ALU.mult,
             )
-            for u in range(B - 1):
+            for u in range(B):
                 chunk, within = divmod((step + u - SKEW) % T, CHUNK)
+                if u == B - 1 and chunk >= SCALAR_CHUNKS:
+                    continue
                 column = chunk * COLS + u * CHUNK + within
                 with nc.allow_low_precision(reason="v is rounded once to bfloat16"):
                     nc.scalar.activation(
@@ -166,7 +170,7 @@ def tile_pamcharecoder_kernel(tc, emb, pe, w1, b1, w2, b2, gamma, beta, offs, ou
                     )
             if step == AHEAD:
                 nc.vector.reciprocal(inv_sum[:, VECTOR_ROWS:], row_sum[:, VECTOR_ROWS:])
-            if (step + 1) % BATCH == 0:
+            if (step + 1) % BATCH == 0 and step >= SCALAR_CHUNKS * CHUNK:
                 nc.vector.tensor_reduce(
                     last_sums[:, step + 1 - BATCH : step + 1],
                     prod[:, step + 1 - BATCH : step + 1, B - 1, :],

@@ -22,7 +22,8 @@ CHUNKS = T // CHUNK
 COLS = B * CHUNK
 STAGES = 5
 SPACING = 2
-VECTOR_ROWS = CHUNK
+LEAD = 2
+EARLY_ROWS = CHUNK
 AHEAD = 12
 BATCH = 8
 SCALAR_CHUNKS = 2
@@ -63,6 +64,8 @@ def tile_pamcharecoder_kernel(tc, emb, pe, w1, b1, w2, b2, gamma, beta, offs, ou
         nc.gpsimd.memset(ones[:], 1.0)
         tiny = held.tile([C, 1], F32, name="tiny")
         nc.gpsimd.memset(tiny[:], TINY)
+        beta_wide = held.tile([C, N], F32, name="beta_wide")
+        nc.gpsimd.memset(beta_wide[:], 0.0)
 
         neg_max = held.tile([C, 1], F32, name="neg_max")
         nc.vector.tensor_reduce(neg_max[:], code[:], axis=AXIS.X, op=ALU.max, negate=True)
@@ -86,12 +89,8 @@ def tile_pamcharecoder_kernel(tc, emb, pe, w1, b1, w2, b2, gamma, beta, offs, ou
                 ACT.Exp,
                 bias=shift[:, i : i + 1],
                 scale=code[:, i : i + 1],
-                accum_out=row_sum[:, e : e + 1] if e >= VECTOR_ROWS else None,
+                accum_out=row_sum[:, e : e + 1],
             )
-        for first in range(0, VECTOR_ROWS, CHUNK):
-            rows = slice(first, first + CHUNK)
-            nc.vector.tensor_reduce(row_sum[:, rows], weights[:, rows, :], axis=AXIS.X, op=ALU.add)
-            nc.vector.reciprocal(inv_sum[:, rows], row_sum[:, rows])
 
         prod = held.tile([C, T, B, T], F32, name="prod")
         unread = held.tile([C, T, B, T], BF16, name="unread")
@@ -107,18 +106,12 @@ def tile_pamcharecoder_kernel(tc, emb, pe, w1, b1, w2, b2, gamma, beta, offs, ou
         std = held.tile([C, N], F32, name="std")
         inv_std = held.tile([C, N], F32, name="inv_std")
         normed = held.tile([C, N], F32, name="normed")
-        scaled = held.tile([C, B, T], F32, name="scaled")
+        shifted = held.tile([C, B, T], F32, name="shifted")
+        result = held.tile([C, B, T], F32, name="result")
 
         def finish(chunk, stage):
             cols = slice(chunk * COLS, (chunk + 1) * COLS)
             if stage == 0:
-                if chunk >= SCALAR_CHUNKS:
-                    nc.vector.tensor_tensor(
-                        v_bf[:, (chunk + 1) * COLS - CHUNK : (chunk + 1) * COLS],
-                        last_sums[:, chunk * CHUNK : (chunk + 1) * CHUNK],
-                        inv_sum[:, SKEW + chunk * CHUNK : SKEW + (chunk + 1) * CHUNK],
-                        ALU.mult,
-                    )
                 nc.tensor.matmul(h_ps[:, cols], w1_sb[:], v_bf[:, cols], start=True, stop=True)
             elif stage == 1:
                 nc.scalar.activation(h_bf[:, cols], h_ps[:, cols], ACT.Relu, bias=b1_sb[:, 0:1])
@@ -139,22 +132,39 @@ def tile_pamcharecoder_kernel(tc, emb, pe, w1, b1, w2, b2, gamma, beta, offs, ou
             nc.vector.tensor_scalar_add(std[:, cols], std[:, cols], EPS)
             nc.vector.reciprocal(inv_std[:, cols], std[:, cols])
             nc.vector.tensor_tensor(normed[:, cols], d_ps[chunk][:], inv_std[:, cols], ALU.mult)
-            nc.vector.tensor_scalar(
-                scaled[:, :, chunk * CHUNK : (chunk + 1) * CHUNK],
+            nc.vector.scalar_tensor_tensor(
+                result[:, :, chunk * CHUNK : (chunk + 1) * CHUNK],
                 normed[:, cols].rearrange("c (u i) -> c u i", u=B),
                 gamma_sb[:, 0:1],
-                beta_sb[:, 0:1],
+                shifted[:, :, chunk * CHUNK : (chunk + 1) * CHUNK],
                 op0=ALU.mult,
                 op1=ALU.add,
             )
 
-        for step in range(T):
+        def look_up(step):
             nc.vector.tensor_tensor(
                 prod[:, step, :, :].rearrange("c u t -> c (u t)"),
                 table[:].indirect(offsets[:]),
                 weights[:, step : step + B, :].rearrange("c e t -> c (e t)"),
                 ALU.mult,
             )
+            if step >= SCALAR_CHUNKS * CHUNK and (step + 1) % BATCH == 0:
+                nc.vector.tensor_reduce(
+                    last_sums[:, step + 1 - BATCH : step + 1],
+                    prod[:, step + 1 - BATCH : step + 1, B - 1, :],
+                    axis=AXIS.X,
+                    op=ALU.add,
+                )
+            if step >= SCALAR_CHUNKS * CHUNK and (step + 1) % CHUNK == 0:
+                chunk = step // CHUNK
+                nc.vector.tensor_tensor(
+                    v_bf[:, (chunk + 1) * COLS - CHUNK : (chunk + 1) * COLS],
+                    last_sums[:, chunk * CHUNK : (chunk + 1) * CHUNK],
+                    inv_sum[:, SKEW + chunk * CHUNK : SKEW + (chunk + 1) * CHUNK],
+                    ALU.mult,
+                )
+
+        def sum_up(step):
             for u in range(B):
                 chunk, within = divmod((step + u - SKEW) % T, CHUNK)
                 if u == B - 1 and chunk >= SCALAR_CHUNKS:
@@ -168,30 +178,31 @@ def tile_pamcharecoder_kernel(tc, emb, pe, w1, b1, w2, b2, gamma, beta, offs, ou
                         scale=inv_sum[:, step + u : step + u + 1],
                         accum_out=v_bf[:, column : column + 1],
                     )
+
+        for ahead in range(T + LEAD):
+            if ahead < T:
+                look_up(ahead)
+            if ahead == LEAD - 1:
+                nc.vector.reciprocal(inv_sum[:, :EARLY_ROWS], row_sum[:, :EARLY_ROWS])
+            step = ahead - LEAD
+            if step >= 0:
+                sum_up(step)
             if step == AHEAD:
-                nc.vector.reciprocal(inv_sum[:, VECTOR_ROWS:], row_sum[:, VECTOR_ROWS:])
-            if (step + 1) % BATCH == 0 and step >= SCALAR_CHUNKS * CHUNK:
-                nc.vector.tensor_reduce(
-                    last_sums[:, step + 1 - BATCH : step + 1],
-                    prod[:, step + 1 - BATCH : step + 1, B - 1, :],
-                    axis=AXIS.X,
-                    op=ALU.add,
-                )
+                nc.vector.reciprocal(inv_sum[:, EARLY_ROWS:], row_sum[:, EARLY_ROWS:])
             chunk, since = divmod(step - (CHUNK + SKEW - 1), CHUNK)
             if chunk >= 0 and since % SPACING == 0 and since // SPACING < STAGES:
                 finish(chunk, since // SPACING)
         finish(CHUNKS - 1, 0)
+        nc.vector.tensor_scalar_add(beta_wide[:], beta_wide[:], beta_sb[:, 0:1])
+        nc.vector.tensor_tensor(
+            shifted[:].rearrange("c u i -> c (u i)"),
+            table[:].indirect(offsets[:]),
+            beta_wide[:],
+            ALU.add,
+        )
         for chunk in range(CHUNKS - 1):
             apply_norm(chunk)
         for stage in range(1, STAGES):
             finish(CHUNKS - 1, stage)
         apply_norm(CHUNKS - 1)
-
-        result = held.tile([C, N], F32, name="result")
-        nc.vector.tensor_tensor(
-            result[:],
-            table[:].indirect(offsets[:]),
-            scaled[:].rearrange("c u i -> c (u i)"),
-            ALU.add,
-        )
-        nc.sync.dma_start(out, result[:])
+        nc.sync.dma_start(out, result[:].rearrange("c u i -> c (u i)"))

@@ -38,6 +38,10 @@ def tile_pamcharecoder_kernel(tc, emb, pe, w1, b1, w2, b2, gamma, beta, offs, ou
         tc.tile_pool(name="held", bufs=1) as held,
         tc.psum_pool(name="psum", bufs=1) as psum,
     ):
+        warm = held.tile([C, 1], F32, name="warm")
+        nc.vector.memset(warm[:], 0.0)
+        nc.scalar.activation(warm[:], warm[:], ACT.Exp)
+
         offsets = held.tile([C, N // 16], U16, name="offsets")
         nc.sync.dma_start(offsets[:], offs)
         code = held.tile([C, T], F32, name="code")

@@ -17,16 +17,12 @@ EPS = 1e-6
 TINY = 1e-30
 SKEW = B - 1
 ROWS = T + SKEW
-CHUNK = 16
-CHUNKS = T // CHUNK
-COLS = B * CHUNK
-STAGES = 5
-SPACING = 2
 LEAD = 2
-EARLY_ROWS = CHUNK
-AHEAD = 12
-BATCH = 8
-SCALAR_CHUNKS = 2
+PE_FROM, PE_TO = 0, 16
+ROW_BLOCK = 17
+SPLIT = 52
+TAIL_FROM = 54
+SPACING = 2
 
 FLOPS = 2 * C * N * T + 2 * 2 * C * C * N
 BYTES = 4 * C * N + 4 * C * T + 2 * 2 * C * C + 4 * 4 * C + 2 * C * (N // 16) + 4 * C * N
@@ -61,9 +57,10 @@ def tile_pamcharecoder_kernel(tc, emb, pe, w1, b1, w2, b2, gamma, beta, offs, ou
         beta_sb = held.tile([C, 1], F32, name="beta_sb")
         nc.sync.dma_start(beta_sb[:], beta)
 
+        identity = held.tile([C, C], F32, name="identity")
+        make_identity(nc, identity[:])
         centre = held.tile([C, C], F32, name="centre")
-        make_identity(nc, centre[:])
-        nc.gpsimd.tensor_scalar_add(centre[:], centre[:], -1.0 / C)
+        nc.gpsimd.tensor_scalar_add(centre[:], identity[:], -1.0 / C)
         ones = held.tile([C, C], F32, name="ones")
         nc.gpsimd.memset(ones[:], 1.0)
         tiny = held.tile([C, 1], F32, name="tiny")
@@ -95,55 +92,14 @@ def tile_pamcharecoder_kernel(tc, emb, pe, w1, b1, w2, b2, gamma, beta, offs, ou
                 scale=code[:, i : i + 1],
                 accum_out=row_sum[:, e : e + 1],
             )
+            if (e + 1) % ROW_BLOCK == 0 or e == ROWS - 1:
+                block = slice(e - e % ROW_BLOCK, e + 1)
+                nc.vector.reciprocal(inv_sum[:, block], row_sum[:, block])
 
         prod = held.tile([C, T, B, T], F32, name="prod")
         unread = held.tile([C, T, B, T], BF16, name="unread")
-        v_bf = held.tile([C, N], BF16, name="v_bf")
-        last_sums = held.tile([C, T], F32, name="last_sums")
-        h_ps = psum.tile([C, N], F32, name="h_ps")
-        h_bf = held.tile([C, N], BF16, name="h_bf")
-        r_ps = psum.tile([C, N], F32, name="r_ps")
-        r_sb = held.tile([C, N], F32, name="r_sb")
-        d_ps = [psum.tile([C, COLS], F32, name=f"d_ps{chunk}") for chunk in range(CHUNKS)]
-        squared = held.tile([C, N], F32, name="squared")
-        ssq_ps = psum.tile([C, N], F32, name="ssq_ps")
-        std = held.tile([C, N], F32, name="std")
-        inv_std = held.tile([C, N], F32, name="inv_std")
-        normed = held.tile([C, N], F32, name="normed")
-        shifted = held.tile([C, B, T], F32, name="shifted")
-        result = held.tile([C, B, T], F32, name="result")
-
-        def finish(chunk, stage):
-            cols = slice(chunk * COLS, (chunk + 1) * COLS)
-            if stage == 0:
-                nc.tensor.matmul(h_ps[:, cols], w1_sb[:], v_bf[:, cols], start=True, stop=True)
-            elif stage == 1:
-                nc.scalar.activation(h_bf[:, cols], h_ps[:, cols], ACT.Relu, bias=b1_sb[:, 0:1])
-                nc.tensor.matmul(r_ps[:, cols], w2_sb[:], h_bf[:, cols], start=True, stop=True)
-            elif stage == 2:
-                nc.scalar.activation(r_sb[:, cols], r_ps[:, cols], ACT.Relu, bias=b2_sb[:, 0:1])
-                nc.tensor.matmul(d_ps[chunk][:], centre[:], r_sb[:, cols], start=True, stop=True)
-            elif stage == 3:
-                nc.scalar.activation(squared[:, cols], d_ps[chunk][:], ACT.Square)
-                nc.tensor.matmul(ssq_ps[:, cols], ones[:], squared[:, cols], start=True, stop=True)
-            elif stage == 4:
-                nc.scalar.activation(
-                    std[:, cols], ssq_ps[:, cols], ACT.Sqrt, bias=tiny[:, 0:1], scale=1.0 / (C - 1)
-                )
-
-        def apply_norm(chunk):
-            cols = slice(chunk * COLS, (chunk + 1) * COLS)
-            nc.vector.tensor_scalar_add(std[:, cols], std[:, cols], EPS)
-            nc.vector.reciprocal(inv_std[:, cols], std[:, cols])
-            nc.vector.tensor_tensor(normed[:, cols], d_ps[chunk][:], inv_std[:, cols], ALU.mult)
-            nc.vector.scalar_tensor_tensor(
-                result[:, :, chunk * CHUNK : (chunk + 1) * CHUNK],
-                normed[:, cols].rearrange("c (u i) -> c u i", u=B),
-                gamma_sb[:, 0:1],
-                shifted[:, :, chunk * CHUNK : (chunk + 1) * CHUNK],
-                op0=ALU.mult,
-                op1=ALU.add,
-            )
+        v_bf = held.tile([C, B, T], BF16, name="v_bf")
+        sums_ps = psum.tile([C, B, PE_TO - PE_FROM], F32, name="sums_ps")
 
         def look_up(step):
             nc.vector.tensor_tensor(
@@ -152,51 +108,119 @@ def tile_pamcharecoder_kernel(tc, emb, pe, w1, b1, w2, b2, gamma, beta, offs, ou
                 weights[:, step : step + B, :].rearrange("c e t -> c (e t)"),
                 ALU.mult,
             )
-            if step >= SCALAR_CHUNKS * CHUNK and (step + 1) % BATCH == 0:
-                nc.vector.tensor_reduce(
-                    last_sums[:, step + 1 - BATCH : step + 1],
-                    prod[:, step + 1 - BATCH : step + 1, B - 1, :],
-                    axis=AXIS.X,
-                    op=ALU.add,
-                )
-            if step >= SCALAR_CHUNKS * CHUNK and (step + 1) % CHUNK == 0:
-                chunk = step // CHUNK
-                nc.vector.tensor_tensor(
-                    v_bf[:, (chunk + 1) * COLS - CHUNK : (chunk + 1) * COLS],
-                    last_sums[:, chunk * CHUNK : (chunk + 1) * CHUNK],
-                    inv_sum[:, SKEW + chunk * CHUNK : SKEW + (chunk + 1) * CHUNK],
-                    ALU.mult,
-                )
 
-        def sum_up(step):
+        def sum_on_scalar(step):
             for u in range(B):
-                chunk, within = divmod((step + u - SKEW) % T, CHUNK)
-                if u == B - 1 and chunk >= SCALAR_CHUNKS:
-                    continue
-                column = chunk * COLS + u * CHUNK + within
                 with nc.allow_low_precision(reason="v is rounded once to bfloat16"):
                     nc.scalar.activation(
                         unread[:, step, u, :],
                         prod[:, step, u, :],
                         ACT.Copy,
                         scale=inv_sum[:, step + u : step + u + 1],
-                        accum_out=v_bf[:, column : column + 1],
+                        accum_out=v_bf[:, u, step : step + 1],
                     )
+
+        def sum_on_tensor():
+            for t in range(T):
+                nc.tensor.matmul(
+                    sums_ps[:],
+                    identity[:],
+                    prod[:, PE_FROM:PE_TO, :, t].rearrange("c s u -> c u s"),
+                    start=(t == 0),
+                    stop=(t == T - 1),
+                )
+
+        def round_tensor_sums():
+            for u in range(B):
+                nc.vector.tensor_tensor(
+                    v_bf[:, u, PE_FROM:PE_TO],
+                    sums_ps[:, u, :],
+                    inv_sum[:, PE_FROM + u : PE_TO + u],
+                    ALU.mult,
+                )
+
+        groups = [slice(0, SPLIT), slice(SPLIT, T)]
+        widths = [B * SPLIT, B * (T - SPLIT)]
+        h_ps = [psum.tile([C, w], F32, name=f"h_ps{g}") for g, w in enumerate(widths)]
+        h_bf = [held.tile([C, w], BF16, name=f"h_bf{g}") for g, w in enumerate(widths)]
+        r_sb = [held.tile([C, w], F32, name=f"r_sb{g}") for g, w in enumerate(widths)]
+        r_ps = psum.tile([C, N], F32, name="r_ps")
+        r_cols = [slice(0, widths[0]), slice(widths[0], N)]
+        d_ps = [psum.tile([C, w], F32, name=f"d_ps{g}") for g, w in enumerate(widths)]
+        squared = [held.tile([C, w], F32, name=f"squared{g}") for g, w in enumerate(widths)]
+        ssq_ps = psum.tile([C, N], F32, name="ssq_ps")
+        std = [held.tile([C, w], F32, name=f"std{g}") for g, w in enumerate(widths)]
+        inv_std = [held.tile([C, w], F32, name=f"inv_std{g}") for g, w in enumerate(widths)]
+        normed = [held.tile([C, w], F32, name=f"normed{g}") for g, w in enumerate(widths)]
+        shifted = held.tile([C, B, T], F32, name="shifted")
+        result = held.tile([C, B, T], F32, name="result")
+
+        def project_1(g):
+            nc.tensor.matmul(h_ps[g][:], w1_sb[:], v_bf[:, :, groups[g]], start=True, stop=True)
+
+        def project_2(g):
+            nc.tensor.matmul(r_ps[:, r_cols[g]], w2_sb[:], h_bf[g][:], start=True, stop=True)
+
+        def deviate(g):
+            nc.tensor.matmul(d_ps[g][:], centre[:], r_sb[g][:], start=True, stop=True)
+
+        def sum_squares(g):
+            nc.scalar.activation(squared[g][:], d_ps[g][:], ACT.Square)
+            nc.tensor.matmul(ssq_ps[:, r_cols[g]], ones[:], squared[g][:], start=True, stop=True)
+
+        def deviation(g):
+            nc.scalar.activation(
+                std[g][:], ssq_ps[:, r_cols[g]], ACT.Sqrt, bias=tiny[:, 0:1], scale=1.0 / (C - 1)
+            )
+
+        def add_norm(g):
+            nc.vector.tensor_scalar_add(std[g][:], std[g][:], EPS)
+            nc.vector.reciprocal(inv_std[g][:], std[g][:])
+            nc.vector.tensor_tensor(normed[g][:], d_ps[g][:], inv_std[g][:], ALU.mult)
+            by_sentence = normed[g][:].rearrange("c (u s) -> c u s", u=B)
+            first, end = groups[g].start, groups[g].stop
+            for u in range(B):
+                wrapped = max(SKEW - u - first, 0)
+                if wrapped:
+                    nc.vector.scalar_tensor_tensor(
+                        result[:, u, T - wrapped :],
+                        by_sentence[:, u, :wrapped],
+                        gamma_sb[:, 0:1],
+                        shifted[:, u, T - wrapped :],
+                        op0=ALU.mult,
+                        op1=ALU.add,
+                    )
+                nc.vector.scalar_tensor_tensor(
+                    result[:, u, first + wrapped + u - SKEW : end + u - SKEW],
+                    by_sentence[:, u, wrapped:],
+                    gamma_sb[:, 0:1],
+                    shifted[:, u, first + wrapped + u - SKEW : end + u - SKEW],
+                    op0=ALU.mult,
+                    op1=ALU.add,
+                )
 
         for ahead in range(T + LEAD):
             if ahead < T:
                 look_up(ahead)
-            if ahead == LEAD - 1:
-                nc.vector.reciprocal(inv_sum[:, :EARLY_ROWS], row_sum[:, :EARLY_ROWS])
+            if ahead == PE_TO:
+                sum_on_tensor()
             step = ahead - LEAD
-            if step >= 0:
-                sum_up(step)
-            if step == AHEAD:
-                nc.vector.reciprocal(inv_sum[:, EARLY_ROWS:], row_sum[:, EARLY_ROWS:])
-            chunk, since = divmod(step - (CHUNK + SKEW - 1), CHUNK)
-            if chunk >= 0 and since % SPACING == 0 and since // SPACING < STAGES:
-                finish(chunk, since // SPACING)
-        finish(CHUNKS - 1, 0)
+            if step >= PE_TO:
+                sum_on_scalar(step)
+            if step == TAIL_FROM:
+                round_tensor_sums()
+                project_1(0)
+            elif step == TAIL_FROM + SPACING:
+                nc.scalar.activation(h_bf[0][:], h_ps[0][:], ACT.Relu, bias=b1_sb[:, 0:1])
+                project_2(0)
+            elif step == TAIL_FROM + 2 * SPACING:
+                nc.scalar.activation(r_sb[0][:], r_ps[:, r_cols[0]], ACT.Relu, bias=b2_sb[:, 0:1])
+                deviate(0)
+            elif step == TAIL_FROM + 3 * SPACING:
+                sum_squares(0)
+
+        project_1(1)
+        deviation(0)
         nc.vector.tensor_scalar_add(beta_wide[:], beta_wide[:], beta_sb[:, 0:1])
         nc.vector.tensor_tensor(
             shifted[:].rearrange("c u i -> c (u i)"),
@@ -204,9 +228,12 @@ def tile_pamcharecoder_kernel(tc, emb, pe, w1, b1, w2, b2, gamma, beta, offs, ou
             beta_wide[:],
             ALU.add,
         )
-        for chunk in range(CHUNKS - 1):
-            apply_norm(chunk)
-        for stage in range(1, STAGES):
-            finish(CHUNKS - 1, stage)
-        apply_norm(CHUNKS - 1)
+        nc.vector.tensor_scalar(h_bf[1][:], h_ps[1][:], b1_sb[:, 0:1], 0.0, op0=ALU.add, op1=ALU.max)
+        project_2(1)
+        nc.vector.tensor_scalar(r_sb[1][:], r_ps[:, r_cols[1]], b2_sb[:, 0:1], 0.0, op0=ALU.add, op1=ALU.max)
+        deviate(1)
+        add_norm(0)
+        sum_squares(1)
+        deviation(1)
+        add_norm(1)
         nc.sync.dma_start(out, result[:].rearrange("c u i -> c (u i)"))

@@ -20,8 +20,9 @@ ROWS = T + SKEW
 LEAD = 2
 PE_FROM, PE_TO = 0, 16
 ROW_BLOCK = 17
-SPLIT = 52
-TAIL_FROM = 54
+LATE = 32
+EARLY = T - LATE
+TAIL_FROM = 50
 SPACING = 2
 
 FLOPS = 2 * C * N * T + 2 * 2 * C * C * N
@@ -63,10 +64,13 @@ def tile_pamcharecoder_kernel(tc, emb, pe, w1, b1, w2, b2, gamma, beta, offs, ou
         nc.gpsimd.tensor_scalar_add(centre[:], identity[:], -1.0 / C)
         ones = held.tile([C, C], F32, name="ones")
         nc.gpsimd.memset(ones[:], 1.0)
+        diag_b2 = held.tile([C, C], F32, name="diag_b2")
+        nc.gpsimd.tensor_scalar_mul(diag_b2[:], identity[:], b2_sb[:, 0:1])
         tiny = held.tile([C, 1], F32, name="tiny")
         nc.gpsimd.memset(tiny[:], TINY)
+        zeros = held.tile([C, N], F32, name="zeros")
+        nc.gpsimd.memset(zeros[:], 0.0)
         beta_wide = held.tile([C, N], F32, name="beta_wide")
-        nc.gpsimd.memset(beta_wide[:], 0.0)
 
         neg_max = held.tile([C, 1], F32, name="neg_max")
         nc.vector.tensor_reduce(neg_max[:], code[:], axis=AXIS.X, op=ALU.max, negate=True)
@@ -95,6 +99,9 @@ def tile_pamcharecoder_kernel(tc, emb, pe, w1, b1, w2, b2, gamma, beta, offs, ou
             if (e + 1) % ROW_BLOCK == 0 or e == ROWS - 1:
                 block = slice(e - e % ROW_BLOCK, e + 1)
                 nc.vector.reciprocal(inv_sum[:, block], row_sum[:, block])
+
+        nc.scalar.activation(warm[:], tiny[:], ACT.Sqrt)
+        nc.scalar.activation(beta_wide[:], zeros[:], ACT.Identity, bias=beta_sb[:, 0:1])
 
         prod = held.tile([C, T, B, T], F32, name="prod")
         unread = held.tile([C, T, B, T], BF16, name="unread")
@@ -139,65 +146,50 @@ def tile_pamcharecoder_kernel(tc, emb, pe, w1, b1, w2, b2, gamma, beta, offs, ou
                     ALU.mult,
                 )
 
-        groups = [slice(0, SPLIT), slice(SPLIT, T)]
-        widths = [B * SPLIT, B * (T - SPLIT)]
-        h_ps = [psum.tile([C, w], F32, name=f"h_ps{g}") for g, w in enumerate(widths)]
-        h_bf = [held.tile([C, w], BF16, name=f"h_bf{g}") for g, w in enumerate(widths)]
-        r_sb = [held.tile([C, w], F32, name=f"r_sb{g}") for g, w in enumerate(widths)]
-        r_ps = psum.tile([C, N], F32, name="r_ps")
-        r_cols = [slice(0, widths[0]), slice(widths[0], N)]
-        d_ps = [psum.tile([C, w], F32, name=f"d_ps{g}") for g, w in enumerate(widths)]
-        squared = [held.tile([C, w], F32, name=f"squared{g}") for g, w in enumerate(widths)]
-        ssq_ps = psum.tile([C, N], F32, name="ssq_ps")
-        std = [held.tile([C, w], F32, name=f"std{g}") for g, w in enumerate(widths)]
-        inv_std = [held.tile([C, w], F32, name=f"inv_std{g}") for g, w in enumerate(widths)]
-        normed = [held.tile([C, w], F32, name=f"normed{g}") for g, w in enumerate(widths)]
+        h_ps = psum.tile([C, B * EARLY], F32, name="h_ps")
+        h_bf = held.tile([C, B * EARLY], BF16, name="h_bf")
+        r_ps = psum.tile([C, B * EARLY], F32, name="r_ps")
+        r_sb = held.tile([C, B * EARLY], F32, name="r_sb")
+        d_ps = psum.tile([C, B * EARLY], F32, name="d_ps")
+        squared = held.tile([C, B * EARLY], F32, name="squared")
+        ssq_ps = psum.tile([C, B * EARLY], F32, name="ssq_ps")
+        std = held.tile([C, B * EARLY], F32, name="std")
+        inv_std = held.tile([C, B * EARLY], F32, name="inv_std")
+        normed = held.tile([C, B * EARLY], F32, name="normed")
         shifted = held.tile([C, B, T], F32, name="shifted")
         result = held.tile([C, B, T], F32, name="result")
 
-        def project_1(g):
-            nc.tensor.matmul(h_ps[g][:], w1_sb[:], v_bf[:, :, groups[g]], start=True, stop=True)
-
-        def project_2(g):
-            nc.tensor.matmul(r_ps[:, r_cols[g]], w2_sb[:], h_bf[g][:], start=True, stop=True)
-
-        def deviate(g):
-            nc.tensor.matmul(d_ps[g][:], centre[:], r_sb[g][:], start=True, stop=True)
-
-        def sum_squares(g):
-            nc.scalar.activation(squared[g][:], d_ps[g][:], ACT.Square)
-            nc.tensor.matmul(ssq_ps[:, r_cols[g]], ones[:], squared[g][:], start=True, stop=True)
-
-        def deviation(g):
-            nc.scalar.activation(
-                std[g][:], ssq_ps[:, r_cols[g]], ACT.Sqrt, bias=tiny[:, 0:1], scale=1.0 / (C - 1)
-            )
-
-        def add_norm(g):
-            nc.vector.tensor_scalar_add(std[g][:], std[g][:], EPS)
-            nc.vector.reciprocal(inv_std[g][:], std[g][:])
-            nc.vector.tensor_tensor(normed[g][:], d_ps[g][:], inv_std[g][:], ALU.mult)
-            by_sentence = normed[g][:].rearrange("c (u s) -> c u s", u=B)
-            first, end = groups[g].start, groups[g].stop
-            for u in range(B):
-                wrapped = max(SKEW - u - first, 0)
-                if wrapped:
-                    nc.vector.scalar_tensor_tensor(
-                        result[:, u, T - wrapped :],
-                        by_sentence[:, u, :wrapped],
-                        gamma_sb[:, 0:1],
-                        shifted[:, u, T - wrapped :],
-                        op0=ALU.mult,
-                        op1=ALU.add,
-                    )
+        def add_normed(u, first, values):
+            wrapped = max(SKEW - u - first, 0)
+            count = values.shape[1]
+            start = first + wrapped + u - SKEW
+            pieces = [(start, wrapped, count)]
+            if wrapped:
+                pieces.append((T - wrapped, 0, wrapped))
+            for position, begin, end in pieces:
                 nc.vector.scalar_tensor_tensor(
-                    result[:, u, first + wrapped + u - SKEW : end + u - SKEW],
-                    by_sentence[:, u, wrapped:],
+                    result[:, u, position : position + end - begin],
+                    values[:, begin:end],
                     gamma_sb[:, 0:1],
-                    shifted[:, u, first + wrapped + u - SKEW : end + u - SKEW],
+                    shifted[:, u, position : position + end - begin],
                     op0=ALU.mult,
                     op1=ALU.add,
                 )
+
+        def early_norm():
+            halves = [slice(0, B // 2 * EARLY), slice(B // 2 * EARLY, B * EARLY)]
+            for half in halves:
+                nc.vector.tensor_scalar_add(std[:, half], std[:, half], EPS)
+            for half in halves:
+                nc.vector.reciprocal(inv_std[:, half], std[:, half])
+            for half in halves:
+                nc.vector.tensor_tensor(normed[:, half], d_ps[:, half], inv_std[:, half], ALU.mult)
+            for u in range(B):
+                add_normed(u, 0, normed[:, u * EARLY : (u + 1) * EARLY])
+
+        late_h_ps = psum.tile([C, B * LATE], F32, name="late_h_ps")
+        late_r_ps = psum.tile([B * LATE, C], F32, name="late_r_ps")
+        nc.tensor.matmul(late_r_ps[:], ones[:], diag_b2[:], start=True, stop=False)
 
         for ahead in range(T + LEAD):
             if ahead < T:
@@ -209,31 +201,51 @@ def tile_pamcharecoder_kernel(tc, emb, pe, w1, b1, w2, b2, gamma, beta, offs, ou
                 sum_on_scalar(step)
             if step == TAIL_FROM:
                 round_tensor_sums()
-                project_1(0)
+                nc.tensor.matmul(h_ps[:], w1_sb[:], v_bf[:, :, :EARLY], start=True, stop=True)
             elif step == TAIL_FROM + SPACING:
-                nc.scalar.activation(h_bf[0][:], h_ps[0][:], ACT.Relu, bias=b1_sb[:, 0:1])
-                project_2(0)
+                nc.scalar.activation(h_bf[:], h_ps[:], ACT.Relu, bias=b1_sb[:, 0:1])
+                nc.tensor.matmul(r_ps[:], w2_sb[:], h_bf[:], start=True, stop=True)
             elif step == TAIL_FROM + 2 * SPACING:
-                nc.scalar.activation(r_sb[0][:], r_ps[:, r_cols[0]], ACT.Relu, bias=b2_sb[:, 0:1])
-                deviate(0)
+                nc.scalar.activation(r_sb[:], r_ps[:], ACT.Relu, bias=b2_sb[:, 0:1])
+                nc.tensor.matmul(d_ps[:], centre[:], r_sb[:], start=True, stop=True)
             elif step == TAIL_FROM + 3 * SPACING:
-                sum_squares(0)
+                nc.scalar.activation(squared[:], d_ps[:], ACT.Square)
+                nc.tensor.matmul(ssq_ps[:], ones[:], squared[:], start=True, stop=True)
+            elif step == TAIL_FROM + 5 * SPACING:
+                nc.scalar.activation(std[:], ssq_ps[:], ACT.Sqrt, bias=tiny[:, 0:1], scale=1.0 / (C - 1))
 
-        project_1(1)
-        deviation(0)
-        nc.vector.tensor_scalar_add(beta_wide[:], beta_wide[:], beta_sb[:, 0:1])
         nc.vector.tensor_tensor(
             shifted[:].rearrange("c u i -> c (u i)"),
             table[:].indirect(offsets[:]),
             beta_wide[:],
             ALU.add,
         )
-        nc.vector.tensor_scalar(h_bf[1][:], h_ps[1][:], b1_sb[:, 0:1], 0.0, op0=ALU.add, op1=ALU.max)
-        project_2(1)
-        nc.vector.tensor_scalar(r_sb[1][:], r_ps[:, r_cols[1]], b2_sb[:, 0:1], 0.0, op0=ALU.add, op1=ALU.max)
-        deviate(1)
-        add_norm(0)
-        sum_squares(1)
-        deviation(1)
-        add_norm(1)
+        early_norm()
+
+        late_h = held.tile([C, B * LATE], BF16, name="late_h")
+        late_r = held.tile([B * LATE, C], F32, name="late_r")
+        moments_by_parity = held.tile([B * LATE, 6], F32, name="moments_by_parity")
+        moments = held.tile([B * LATE, 2], F32, name="moments")
+        late_std = held.tile([B * LATE, 1], F32, name="late_std")
+        late_inv = held.tile([B * LATE, 1], F32, name="late_inv")
+        late_n = held.tile([B * LATE, C], F32, name="late_n")
+        late_ps = psum.tile([C, B * LATE], F32, name="late_ps")
+
+        nc.tensor.matmul(late_h_ps[:], w1_sb[:], v_bf[:, :, EARLY:], start=True, stop=True)
+        nc.scalar.activation(late_h[:], late_h_ps[:], ACT.Relu, bias=b1_sb[:, 0:1])
+        nc.tensor.matmul(late_r_ps[:], late_h[:], w2_sb[:], start=False, stop=True)
+        nc.scalar.activation(late_r[:], late_r_ps[:], ACT.Relu)
+        nc.vector.bn_stats(moments_by_parity[:], late_r[:])
+        nc.vector.bn_aggr(moments[:], moments_by_parity[:])
+        nc.scalar.activation(
+            late_std[:], moments[:, 1:2], ACT.Sqrt, bias=tiny[:, 0:1], scale=C / (C - 1)
+        )
+        nc.vector.tensor_scalar_add(late_std[:], late_std[:], EPS)
+        nc.vector.reciprocal(late_inv[:], late_std[:])
+        nc.vector.tensor_scalar(
+            late_n[:], late_r[:], moments[:, 0:1], late_inv[:, 0:1], op0=ALU.subtract, op1=ALU.mult
+        )
+        nc.tensor.matmul(late_ps[:], late_n[:], identity[:], start=True, stop=True)
+        for u in range(B):
+            add_normed(u, EARLY, late_ps[:, u * LATE : (u + 1) * LATE])
         nc.sync.dma_start(out, result[:].rearrange("c u i -> c (u i)"))

@@ -63,13 +63,12 @@ def tile_pamcharecoder_kernel(tc, emb, pe, w1, b1, w2, b2, gamma, beta, offs, ou
         centre = held.tile([C, C], F32, name="centre")
         nc.gpsimd.tensor_scalar_add(centre[:], identity[:], -1.0 / C)
         ones = held.tile([C, C], F32, name="ones")
-        nc.gpsimd.memset(ones[:], 1.0)
+        nc.vector.memset(ones[:], 1.0)
         diag_b2 = held.tile([C, C], F32, name="diag_b2")
-        nc.gpsimd.tensor_scalar_mul(diag_b2[:], identity[:], b2_sb[:, 0:1])
         tiny = held.tile([C, 1], F32, name="tiny")
-        nc.gpsimd.memset(tiny[:], TINY)
+        nc.vector.memset(tiny[:], TINY)
         zeros = held.tile([C, N], F32, name="zeros")
-        nc.gpsimd.memset(zeros[:], 0.0)
+        nc.vector.memset(zeros[:], 0.0)
         beta_wide = held.tile([C, N], F32, name="beta_wide")
 
         neg_max = held.tile([C, 1], F32, name="neg_max")
@@ -102,6 +101,7 @@ def tile_pamcharecoder_kernel(tc, emb, pe, w1, b1, w2, b2, gamma, beta, offs, ou
 
         nc.scalar.activation(warm[:], tiny[:], ACT.Sqrt)
         nc.scalar.activation(beta_wide[:], zeros[:], ACT.Identity, bias=beta_sb[:, 0:1])
+        nc.scalar.activation(diag_b2[:], identity[:], ACT.Copy, scale=b2_sb[:, 0:1])
 
         prod = held.tile([C, T, B, T], F32, name="prod")
         unread = held.tile([C, T, B, T], BF16, name="unread")

@@ -99,7 +99,7 @@ def tile_pamcharecoder_kernel(tc, emb, pe, w1, b1, w2, b2, gamma, beta, offs, ou
                 block = slice(e - e % ROW_BLOCK, e + 1)
                 nc.vector.reciprocal(inv_sum[:, block], row_sum[:, block])
 
-        nc.scalar.activation(warm[:], tiny[:], ACT.Sqrt)
+        nc.scalar.activation(warm[:], row_sum[:, ROWS - 1 :], ACT.Sqrt)
         nc.scalar.activation(beta_wide[:], zeros[:], ACT.Identity, bias=beta_sb[:, 0:1])
         nc.scalar.activation(diag_b2[:], identity[:], ACT.Copy, scale=b2_sb[:, 0:1])
 

@@ -225,7 +225,9 @@ def tile_pamcharecoder_kernel(tc, emb, pe, w1, b1, w2, b2, gamma, beta, offs, ou
         late_h = held.tile([C, B * LATE], BF16, name="late_h")
         late_r = held.tile([B * LATE, C], F32, name="late_r")
         moments_by_parity = held.tile([B * LATE, 6], F32, name="moments_by_parity")
-        moments = held.tile([B * LATE, 2], F32, name="moments")
+        moments = held.tile([B * LATE, 3], F32, name="moments")
+        nc.vector.memset(moments[:, 2:3], EPS * EPS * (C - 1) / C)
+        roots = held.tile([B * LATE, 2], F32, name="roots")
         late_std = held.tile([B * LATE, 1], F32, name="late_std")
         late_inv = held.tile([B * LATE, 1], F32, name="late_inv")
         late_n = held.tile([B * LATE, C], F32, name="late_n")
@@ -236,16 +238,15 @@ def tile_pamcharecoder_kernel(tc, emb, pe, w1, b1, w2, b2, gamma, beta, offs, ou
         nc.tensor.matmul(late_r_ps[:], late_h[:], w2_sb[:], start=False, stop=True)
         nc.scalar.activation(late_r[:], late_r_ps[:], ACT.Relu)
         nc.vector.bn_stats(moments_by_parity[:], late_r[:])
-        nc.vector.bn_aggr(moments[:], moments_by_parity[:])
+        nc.vector.bn_aggr(moments[:, 0:2], moments_by_parity[:])
         nc.scalar.activation(
-            late_std[:], moments[:, 1:2], ACT.Sqrt, bias=tiny[:, 0:1], scale=C / (C - 1)
+            roots[:], moments[:, 1:3], ACT.Sqrt, bias=tiny[:, 0:1], scale=C / (C - 1), accum_out=late_std[:]
         )
-        nc.vector.tensor_scalar_add(late_std[:], late_std[:], EPS)
         nc.vector.reciprocal(late_inv[:], late_std[:])
         nc.vector.tensor_scalar(
             late_n[:], late_r[:], moments[:, 0:1], late_inv[:, 0:1], op0=ALU.subtract, op1=ALU.mult
         )
-        nc.tensor.matmul(late_ps[:], late_n[:], identity[:], start=True, stop=True)
+        nc.tensor.transpose(late_ps[:], late_n[:], identity[:])
         for u in range(B):
             add_normed(u, EARLY, late_ps[:, u * LATE : (u + 1) * LATE])
         nc.sync.dma_start(out, result[:].rearrange("c u i -> c (u i)"))

@@ -20,10 +20,10 @@ ROWS = T + SKEW
 LEAD = 2
 PE_FROM, PE_TO = 0, 16
 ROW_BLOCK = 17
-LATE = 32
-EARLY = T - LATE
+GROUP = C // B
+GROUPS = T // GROUP
 TAIL_FROM = 50
-SPACING = 2
+SPACING = 4
 
 FLOPS = 2 * C * N * T + 2 * 2 * C * C * N
 BYTES = 4 * C * N + 4 * C * T + 2 * 2 * C * C + 4 * 4 * C + 2 * C * (N // 16) + 4 * C * N
@@ -60,8 +60,6 @@ def tile_pamcharecoder_kernel(tc, emb, pe, w1, b1, w2, b2, gamma, beta, offs, ou
 
         identity = held.tile([C, C], F32, name="identity")
         make_identity(nc, identity[:])
-        centre = held.tile([C, C], F32, name="centre")
-        nc.gpsimd.tensor_scalar_add(centre[:], identity[:], -1.0 / C)
         ones = held.tile([C, C], F32, name="ones")
         nc.vector.memset(ones[:], 1.0)
         diag_b2 = held.tile([C, C], F32, name="diag_b2")
@@ -146,50 +144,78 @@ def tile_pamcharecoder_kernel(tc, emb, pe, w1, b1, w2, b2, gamma, beta, offs, ou
                     ALU.mult,
                 )
 
-        h_ps = psum.tile([C, B * EARLY], F32, name="h_ps")
-        h_bf = held.tile([C, B * EARLY], BF16, name="h_bf")
-        r_ps = psum.tile([C, B * EARLY], F32, name="r_ps")
-        r_sb = held.tile([C, B * EARLY], F32, name="r_sb")
-        d_ps = psum.tile([C, B * EARLY], F32, name="d_ps")
-        squared = held.tile([C, B * EARLY], F32, name="squared")
-        ssq_ps = psum.tile([C, B * EARLY], F32, name="ssq_ps")
-        std = held.tile([C, B * EARLY], F32, name="std")
-        inv_std = held.tile([C, B * EARLY], F32, name="inv_std")
-        normed = held.tile([C, B * EARLY], F32, name="normed")
+        tail = range(GROUPS)
+        h_ps = [psum.tile([C, C], F32, name=f"h_ps{g}") for g in tail]
+        h_bf = [held.tile([C, C], BF16, name=f"h_bf{g}") for g in tail]
+        r_ps = [psum.tile([C, C], F32, name=f"r_ps{g}") for g in tail]
+        r_sb = [held.tile([C, C], F32, name=f"r_sb{g}") for g in tail]
+        r_sum = [held.tile([C, 1], F32, name=f"r_sum{g}") for g in tail]
+        mean = [held.tile([C, 1], F32, name=f"mean{g}") for g in tail]
+        squares = [held.tile([C, C], F32, name=f"squares{g}") for g in tail]
+        square_sums = [held.tile([C, 2], F32, name=f"square_sums{g}") for g in tail]
+        roots = [held.tile([C, 2], F32, name=f"roots{g}") for g in tail]
+        std_eps = [held.tile([C, 1], F32, name=f"std_eps{g}") for g in tail]
+        inv_std = [held.tile([C, 1], F32, name=f"inv_std{g}") for g in tail]
+        normed = [held.tile([C, C], F32, name=f"normed{g}") for g in tail]
         shifted = held.tile([C, B, T], F32, name="shifted")
         result = held.tile([C, B, T], F32, name="result")
+        for g in tail:
+            nc.vector.memset(square_sums[g][:, 1:2], EPS * EPS * (C - 1) * C * C)
+            nc.tensor.matmul(r_ps[g][:], ones[:], diag_b2[:], start=True, stop=False)
 
-        def add_normed(u, first, values):
-            wrapped = max(SKEW - u - first, 0)
-            count = values.shape[1]
-            start = first + wrapped + u - SKEW
-            pieces = [(start, wrapped, count)]
-            if wrapped:
-                pieces.append((T - wrapped, 0, wrapped))
-            for position, begin, end in pieces:
-                nc.vector.scalar_tensor_tensor(
-                    result[:, u, position : position + end - begin],
-                    values[:, begin:end],
-                    gamma_sb[:, 0:1],
-                    shifted[:, u, position : position + end - begin],
-                    op0=ALU.mult,
-                    op1=ALU.add,
-                )
+        def project_1(g):
+            nc.tensor.matmul(h_ps[g][:], w1_sb[:], v_bf[:, :, g * GROUP : (g + 1) * GROUP], start=True, stop=True)
 
-        def early_norm():
-            halves = [slice(0, B // 2 * EARLY), slice(B // 2 * EARLY, B * EARLY)]
-            for half in halves:
-                nc.vector.tensor_scalar_add(std[:, half], std[:, half], EPS)
-            for half in halves:
-                nc.vector.reciprocal(inv_std[:, half], std[:, half])
-            for half in halves:
-                nc.vector.tensor_tensor(normed[:, half], d_ps[:, half], inv_std[:, half], ALU.mult)
+        def project_2(g):
+            nc.scalar.activation(h_bf[g][:], h_ps[g][:], ACT.Relu, bias=b1_sb[:, 0:1])
+            nc.tensor.matmul(r_ps[g][:], h_bf[g][:], w2_sb[:], start=False, stop=True)
+
+        def statistics(g):
+            nc.scalar.activation(r_sb[g][:], r_ps[g][:], ACT.Relu, accum_out=r_sum[g][:])
+            nc.scalar.activation(
+                squares[g][:],
+                r_sb[g][:],
+                ACT.Square,
+                bias=r_sum[g][:, 0:1],
+                scale=-float(C),
+                accum_out=square_sums[g][:, 0:1],
+            )
+            nc.vector.tensor_scalar_mul(mean[g][:], r_sum[g][:], 1.0 / C)
+            nc.scalar.activation(
+                roots[g][:],
+                square_sums[g][:],
+                ACT.Sqrt,
+                bias=tiny[:, 0:1],
+                scale=1.0 / ((C - 1) * C * C),
+                accum_out=std_eps[g][:],
+            )
+
+        def normalise(g):
+            nc.vector.reciprocal(inv_std[g][:], std_eps[g][:])
+            nc.vector.tensor_scalar(
+                normed[g][:], r_sb[g][:], mean[g][:, 0:1], inv_std[g][:, 0:1], op0=ALU.subtract, op1=ALU.mult
+            )
+
+        def turn_back(g, bank):
+            normed_ps = psum.tile([C, C], F32, name=f"normed_ps{g}", tag=bank)
+            nc.tensor.transpose(normed_ps[:], normed[g][:], identity[:])
+            return normed_ps
+
+        def add_residual(g, normed_ps):
             for u in range(B):
-                add_normed(u, 0, normed[:, u * EARLY : (u + 1) * EARLY])
-
-        late_h_ps = psum.tile([C, B * LATE], F32, name="late_h_ps")
-        late_r_ps = psum.tile([B * LATE, C], F32, name="late_r_ps")
-        nc.tensor.matmul(late_r_ps[:], ones[:], diag_b2[:], start=True, stop=False)
+                wrapped = max(SKEW - u - g * GROUP, 0)
+                pieces = [(g * GROUP + wrapped + u - SKEW, wrapped, GROUP)]
+                if wrapped:
+                    pieces.append((T - wrapped, 0, wrapped))
+                for position, begin, end in pieces:
+                    nc.vector.scalar_tensor_tensor(
+                        result[:, u, position : position + end - begin],
+                        normed_ps[:, u * GROUP + begin : u * GROUP + end],
+                        gamma_sb[:, 0:1],
+                        shifted[:, u, position : position + end - begin],
+                        op0=ALU.mult,
+                        op1=ALU.add,
+                    )
 
         for ahead in range(T + LEAD):
             if ahead < T:
@@ -201,52 +227,23 @@ def tile_pamcharecoder_kernel(tc, emb, pe, w1, b1, w2, b2, gamma, beta, offs, ou
                 sum_on_scalar(step)
             if step == TAIL_FROM:
                 round_tensor_sums()
-                nc.tensor.matmul(h_ps[:], w1_sb[:], v_bf[:, :, :EARLY], start=True, stop=True)
+                project_1(0)
             elif step == TAIL_FROM + SPACING:
-                nc.scalar.activation(h_bf[:], h_ps[:], ACT.Relu, bias=b1_sb[:, 0:1])
-                nc.tensor.matmul(r_ps[:], w2_sb[:], h_bf[:], start=True, stop=True)
+                project_2(0)
             elif step == TAIL_FROM + 2 * SPACING:
-                nc.scalar.activation(r_sb[:], r_ps[:], ACT.Relu, bias=b2_sb[:, 0:1])
-                nc.tensor.matmul(d_ps[:], centre[:], r_sb[:], start=True, stop=True)
-            elif step == TAIL_FROM + 3 * SPACING:
-                nc.scalar.activation(squared[:], d_ps[:], ACT.Square)
-                nc.tensor.matmul(ssq_ps[:], ones[:], squared[:], start=True, stop=True)
-            elif step == TAIL_FROM + 5 * SPACING:
-                nc.scalar.activation(std[:], ssq_ps[:], ACT.Sqrt, bias=tiny[:, 0:1], scale=1.0 / (C - 1))
+                statistics(0)
 
+        project_1(1)
         nc.vector.tensor_tensor(
             shifted[:].rearrange("c u i -> c (u i)"),
             table[:].indirect(offsets[:]),
             beta_wide[:],
             ALU.add,
         )
-        early_norm()
-
-        late_h = held.tile([C, B * LATE], BF16, name="late_h")
-        late_r = held.tile([B * LATE, C], F32, name="late_r")
-        moments_by_parity = held.tile([B * LATE, 6], F32, name="moments_by_parity")
-        moments = held.tile([B * LATE, 3], F32, name="moments")
-        nc.vector.memset(moments[:, 2:3], EPS * EPS * (C - 1) / C)
-        roots = held.tile([B * LATE, 2], F32, name="roots")
-        late_std = held.tile([B * LATE, 1], F32, name="late_std")
-        late_inv = held.tile([B * LATE, 1], F32, name="late_inv")
-        late_n = held.tile([B * LATE, C], F32, name="late_n")
-        late_ps = psum.tile([C, B * LATE], F32, name="late_ps")
-
-        nc.tensor.matmul(late_h_ps[:], w1_sb[:], v_bf[:, :, EARLY:], start=True, stop=True)
-        nc.scalar.activation(late_h[:], late_h_ps[:], ACT.Relu, bias=b1_sb[:, 0:1])
-        nc.tensor.matmul(late_r_ps[:], late_h[:], w2_sb[:], start=False, stop=True)
-        nc.scalar.activation(late_r[:], late_r_ps[:], ACT.Relu)
-        nc.vector.bn_stats(moments_by_parity[:], late_r[:])
-        nc.vector.bn_aggr(moments[:, 0:2], moments_by_parity[:])
-        nc.scalar.activation(
-            roots[:], moments[:, 1:3], ACT.Sqrt, bias=tiny[:, 0:1], scale=C / (C - 1), accum_out=late_std[:]
-        )
-        nc.vector.reciprocal(late_inv[:], late_std[:])
-        nc.vector.tensor_scalar(
-            late_n[:], late_r[:], moments[:, 0:1], late_inv[:, 0:1], op0=ALU.subtract, op1=ALU.mult
-        )
-        nc.tensor.transpose(late_ps[:], late_n[:], identity[:])
-        for u in range(B):
-            add_normed(u, EARLY, late_ps[:, u * LATE : (u + 1) * LATE])
+        normalise(0)
+        project_2(1)
+        add_residual(0, turn_back(0, "h_ps1"))
+        statistics(1)
+        normalise(1)
+        add_residual(1, turn_back(1, "h_ps0"))
         nc.sync.dma_start(out, result[:].rearrange("c u i -> c (u i)"))

@@ -19,7 +19,7 @@ SKEW = B - 1
 ROWS = T + SKEW
 LEAD = 2
 PE_FROM, PE_TO = 0, 16
-ROW_BLOCK = 17
+SQRT_AT = 24
 GROUP = C // B
 GROUPS = T // GROUP
 TAIL_FROM = 50
@@ -93,11 +93,9 @@ def tile_pamcharecoder_kernel(tc, emb, pe, w1, b1, w2, b2, gamma, beta, offs, ou
                 scale=code[:, i : i + 1],
                 accum_out=row_sum[:, e : e + 1],
             )
-            if (e + 1) % ROW_BLOCK == 0 or e == ROWS - 1:
-                block = slice(e - e % ROW_BLOCK, e + 1)
-                nc.vector.reciprocal(inv_sum[:, block], row_sum[:, block])
-
-        nc.scalar.activation(warm[:], row_sum[:, ROWS - 1 :], ACT.Sqrt)
+        log_sum = held.tile([C, ROWS], F32, name="log_sum")
+        nc.scalar.activation(log_sum[:], row_sum[:], ACT.Ln)
+        nc.scalar.activation(inv_sum[:], log_sum[:], ACT.Exp, scale=-1.0)
         nc.scalar.activation(beta_wide[:], zeros[:], ACT.Identity, bias=beta_sb[:, 0:1])
         nc.scalar.activation(diag_b2[:], identity[:], ACT.Copy, scale=b2_sb[:, 0:1])
 
@@ -225,6 +223,8 @@ def tile_pamcharecoder_kernel(tc, emb, pe, w1, b1, w2, b2, gamma, beta, offs, ou
             step = ahead - LEAD
             if step >= PE_TO:
                 sum_on_scalar(step)
+            if step == SQRT_AT:
+                nc.scalar.activation(warm[:], unread[:, step, 0, 0:1], ACT.Sqrt, bias=tiny[:, 0:1], scale=0.0)
             if step == TAIL_FROM:
                 round_tensor_sums()
                 project_1(0)

@@ -19,6 +19,8 @@ SKEW = B - 1
 ROWS = T + SKEW
 LEAD = 2
 PE_FROM, PE_TO = 0, 16
+WARM_FROM = 56
+WARM_LOOK_UPS = 2
 SQRT_AT = 24
 GROUP = C // B
 GROUPS = T // GROUP
@@ -215,6 +217,21 @@ def tile_pamcharecoder_kernel(tc, emb, pe, w1, b1, w2, b2, gamma, beta, offs, ou
                         op1=ALU.add,
                     )
 
+        warm_ps = psum.tile([C, WARM_LOOK_UPS * N], F32, name="warm_ps")
+
+        def warm_by_look_ups(step):
+            nc.tensor.matmul(
+                warm_ps[:],
+                w2_sb[:],
+                unread[:, step + 1 - WARM_LOOK_UPS : step + 1, :, :].rearrange("c s u t -> c (s u t)"),
+                start=True,
+                stop=True,
+            )
+
+        def warm_by_group(g):
+            for part in range(2 * WARM_LOOK_UPS * N // C):
+                nc.tensor.matmul(warm_ps[:, :C], w2_sb[:], h_bf[g][:], start=True, stop=True)
+
         for ahead in range(T + LEAD):
             if ahead < T:
                 look_up(ahead)
@@ -225,6 +242,8 @@ def tile_pamcharecoder_kernel(tc, emb, pe, w1, b1, w2, b2, gamma, beta, offs, ou
                 sum_on_scalar(step)
             if step == SQRT_AT:
                 nc.scalar.activation(warm[:], unread[:, step, 0, 0:1], ACT.Sqrt, bias=tiny[:, 0:1], scale=0.0)
+            if WARM_FROM <= step < T - 1:
+                warm_by_look_ups(step)
             if step == TAIL_FROM:
                 round_tensor_sums()
                 project_1(0)
@@ -243,6 +262,7 @@ def tile_pamcharecoder_kernel(tc, emb, pe, w1, b1, w2, b2, gamma, beta, offs, ou
         normalise(0)
         project_2(1)
         add_residual(0, turn_back(0, "h_ps1"))
+        warm_by_group(1)
         statistics(1)
         normalise(1)
         add_residual(1, turn_back(1, "h_ps0"))

@@ -106,11 +106,11 @@ def tile_pamcharecoder_kernel(tc, emb, pe, w1, b1, w2, b2, gamma, beta, offs, ou
         v_bf = held.tile([C, B, T], BF16, name="v_bf")
         sums_ps = psum.tile([C, B, PE_TO - PE_FROM], F32, name="sums_ps")
 
-        def look_up(step):
+        def look_up(step, u0, u1):
             nc.vector.tensor_tensor(
-                prod[:, step, :, :].rearrange("c u t -> c (u t)"),
-                table[:].indirect(offsets[:]),
-                weights[:, step : step + B, :].rearrange("c e t -> c (e t)"),
+                prod[:, step, u0:u1, :].rearrange("c u t -> c (u t)"),
+                table[:].indirect(offsets[:, u0 * T // 16 : u1 * T // 16]),
+                weights[:, step + u0 : step + u1, :].rearrange("c e t -> c (e t)"),
                 ALU.mult,
             )
 
@@ -233,8 +233,11 @@ def tile_pamcharecoder_kernel(tc, emb, pe, w1, b1, w2, b2, gamma, beta, offs, ou
                 nc.tensor.matmul(warm_ps[:, :C], w2_sb[:], h_bf[g][:], start=True, stop=True)
 
         for ahead in range(T + LEAD):
-            if ahead < T:
-                look_up(ahead)
+            if ahead < T - 1:
+                look_up(ahead, 0, B)
+            elif ahead == T - 1:
+                look_up(ahead, 0, B // 2)
+                look_up(ahead, B // 2, B)
             if ahead == PE_TO:
                 sum_on_tensor()
             step = ahead - LEAD

@@ -25,7 +25,8 @@ SQRT_AT = 24
 GROUP = C // B
 GROUPS = T // GROUP
 TAIL_FROM = 50
-SPACING = 4
+RELU_AT = 55
+STATISTICS_AT = 58
 
 FLOPS = 2 * C * N * T + 2 * 2 * C * C * N
 BYTES = 4 * C * N + 4 * C * T + 2 * 2 * C * C + 4 * 4 * C + 2 * C * (N // 16) + 4 * C * N
@@ -250,9 +251,9 @@ def tile_pamcharecoder_kernel(tc, emb, pe, w1, b1, w2, b2, gamma, beta, offs, ou
             if step == TAIL_FROM:
                 round_tensor_sums()
                 project_1(0)
-            elif step == TAIL_FROM + SPACING:
+            elif step == RELU_AT:
                 project_2(0)
-            elif step == TAIL_FROM + 2 * SPACING:
+            elif step == STATISTICS_AT:
                 statistics(0)
 
         project_1(1)

import concourse.mybir as mybir
from concourse.masks import make_identity

F32 = mybir.dt.float32
BF16 = mybir.dt.bfloat16
U16 = mybir.dt.uint16
ALU = mybir.AluOpType
ACT = mybir.ActivationFunctionType
AXIS = mybir.AxisListType

C = 128
S = 2048
B = 4
T = 64
N = B * T
EPS = 1e-6
TINY = 1e-30
SKEW = B - 1
ROWS = T + SKEW
LEAD = 2
PE_FROM, PE_TO = 0, 16
WARM_FROM = 56
WARM_LOOK_UPS = 2
SQRT_AT = 24
GROUP = C // B
GROUPS = T // GROUP
TAIL_FROM = 50
RELU_AT = 55
STATISTICS_AT = 58

FLOPS = 2 * C * N * T + 2 * 2 * C * C * N
BYTES = 4 * C * N + 4 * C * T + 2 * 2 * C * C + 4 * 4 * C + 2 * C * (N // 16) + 4 * C * N


def tile_pamcharecoder_kernel(tc, emb, pe, w1, b1, w2, b2, gamma, beta, offs, out):
    nc = tc.nc
    with (
        tc.tile_pool(name="held", bufs=1) as held,
        tc.psum_pool(name="psum", bufs=1) as psum,
    ):
        warm = held.tile([C, 1], F32, name="warm")
        nc.vector.memset(warm[:], 0.0)
        nc.scalar.activation(warm[:], warm[:], ACT.Exp)

        offsets = held.tile([C, N // 16], U16, name="offsets")
        nc.sync.dma_start(offsets[:], offs)
        code = held.tile([C, T], F32, name="code")
        nc.scalar.dma_start(code[:], pe)
        table = held.tile([C, S], F32, name="table")
        nc.sync.dma_start(table[:], emb)
        w1_sb = held.tile([C, C], BF16, name="w1_sb")
        nc.sync.dma_start(w1_sb[:], w1)
        w2_sb = held.tile([C, C], BF16, name="w2_sb")
        nc.sync.dma_start(w2_sb[:], w2)
        b1_sb = held.tile([C, 1], F32, name="b1_sb")
        nc.sync.dma_start(b1_sb[:], b1)
        b2_sb = held.tile([C, 1], F32, name="b2_sb")
        nc.sync.dma_start(b2_sb[:], b2)
        gamma_sb = held.tile([C, 1], F32, name="gamma_sb")
        nc.sync.dma_start(gamma_sb[:], gamma)
        beta_sb = held.tile([C, 1], F32, name="beta_sb")
        nc.sync.dma_start(beta_sb[:], beta)

        identity = held.tile([C, C], F32, name="identity")
        make_identity(nc, identity[:])
        ones = held.tile([C, C], F32, name="ones")
        nc.vector.memset(ones[:], 1.0)
        diag_b2 = held.tile([C, C], F32, name="diag_b2")
        tiny = held.tile([C, 1], F32, name="tiny")
        nc.vector.memset(tiny[:], TINY)
        zeros = held.tile([C, N], F32, name="zeros")
        nc.vector.memset(zeros[:], 0.0)
        beta_wide = held.tile([C, N], F32, name="beta_wide")

        neg_max = held.tile([C, 1], F32, name="neg_max")
        nc.vector.tensor_reduce(neg_max[:], code[:], axis=AXIS.X, op=ALU.max, negate=True)
        neg_min = held.tile([C, 1], F32, name="neg_min")
        nc.vector.tensor_reduce(neg_min[:], code[:], axis=AXIS.X, op=ALU.min, negate=True)
        by_max = held.tile([C, T], F32, name="by_max")
        nc.vector.tensor_scalar_mul(by_max[:], code[:], neg_max[:, 0:1])
        shift = held.tile([C, T], F32, name="shift")
        nc.vector.scalar_tensor_tensor(
            shift[:], code[:], neg_min[:, 0:1], by_max[:], op0=ALU.mult, op1=ALU.min
        )

        weights = held.tile([C, ROWS, T], F32, name="weights")
        row_sum = held.tile([C, ROWS], F32, name="row_sum")
        inv_sum = held.tile([C, ROWS], F32, name="inv_sum")
        for e in range(ROWS):
            i = (e - SKEW) % T
            nc.scalar.activation(
                weights[:, e, :],
                code[:],
                ACT.Exp,
                bias=shift[:, i : i + 1],
                scale=code[:, i : i + 1],
                accum_out=row_sum[:, e : e + 1],
            )
        log_sum = held.tile([C, ROWS], F32, name="log_sum")
        nc.scalar.activation(log_sum[:], row_sum[:], ACT.Ln)
        nc.scalar.activation(inv_sum[:], log_sum[:], ACT.Exp, scale=-1.0)
        nc.scalar.activation(beta_wide[:], zeros[:], ACT.Identity, bias=beta_sb[:, 0:1])
        nc.scalar.activation(diag_b2[:], identity[:], ACT.Copy, scale=b2_sb[:, 0:1])

        prod = held.tile([C, T, B, T], F32, name="prod")
        unread = held.tile([C, T, B, T], BF16, name="unread")
        v_bf = held.tile([C, B, T], BF16, name="v_bf")
        sums_ps = psum.tile([C, B, PE_TO - PE_FROM], F32, name="sums_ps")

        def look_up(step, u0, u1):
            nc.vector.tensor_tensor(
                prod[:, step, u0:u1, :].rearrange("c u t -> c (u t)"),
                table[:].indirect(offsets[:, u0 * T // 16 : u1 * T // 16]),
                weights[:, step + u0 : step + u1, :].rearrange("c e t -> c (e t)"),
                ALU.mult,
            )

        def sum_on_scalar(step):
            for u in range(B):
                with nc.allow_low_precision(reason="v is rounded once to bfloat16"):
                    nc.scalar.activation(
                        unread[:, step, u, :],
                        prod[:, step, u, :],
                        ACT.Copy,
                        scale=inv_sum[:, step + u : step + u + 1],
                        accum_out=v_bf[:, u, step : step + 1],
                    )

        def sum_on_tensor():
            for t in range(T):
                nc.tensor.matmul(
                    sums_ps[:],
                    identity[:],
                    prod[:, PE_FROM:PE_TO, :, t].rearrange("c s u -> c u s"),
                    start=(t == 0),
                    stop=(t == T - 1),
                )

        def round_tensor_sums():
            for u in range(B):
                nc.vector.tensor_tensor(
                    v_bf[:, u, PE_FROM:PE_TO],
                    sums_ps[:, u, :],
                    inv_sum[:, PE_FROM + u : PE_TO + u],
                    ALU.mult,
                )

        tail = range(GROUPS)
        h_ps = [psum.tile([C, C], F32, name=f"h_ps{g}") for g in tail]
        h_bf = [held.tile([C, C], BF16, name=f"h_bf{g}") for g in tail]
        r_ps = [psum.tile([C, C], F32, name=f"r_ps{g}") for g in tail]
        r_sb = [held.tile([C, C], F32, name=f"r_sb{g}") for g in tail]
        r_sum = [held.tile([C, 1], F32, name=f"r_sum{g}") for g in tail]
        mean = [held.tile([C, 1], F32, name=f"mean{g}") for g in tail]
        squares = [held.tile([C, C], F32, name=f"squares{g}") for g in tail]
        square_sums = [held.tile([C, 2], F32, name=f"square_sums{g}") for g in tail]
        roots = [held.tile([C, 2], F32, name=f"roots{g}") for g in tail]
        std_eps = [held.tile([C, 1], F32, name=f"std_eps{g}") for g in tail]
        inv_std = [held.tile([C, 1], F32, name=f"inv_std{g}") for g in tail]
        normed = [held.tile([C, C], F32, name=f"normed{g}") for g in tail]
        shifted = held.tile([C, B, T], F32, name="shifted")
        result = held.tile([C, B, T], F32, name="result")
        for g in tail:
            nc.vector.memset(square_sums[g][:, 1:2], EPS * EPS * (C - 1) * C * C)
            nc.tensor.matmul(r_ps[g][:], ones[:], diag_b2[:], start=True, stop=False)

        def project_1(g):
            nc.tensor.matmul(h_ps[g][:], w1_sb[:], v_bf[:, :, g * GROUP : (g + 1) * GROUP], start=True, stop=True)

        def project_2(g):
            nc.scalar.activation(h_bf[g][:], h_ps[g][:], ACT.Relu, bias=b1_sb[:, 0:1])
            nc.tensor.matmul(r_ps[g][:], h_bf[g][:], w2_sb[:], start=False, stop=True)

        def statistics(g):
            nc.scalar.activation(r_sb[g][:], r_ps[g][:], ACT.Relu, accum_out=r_sum[g][:])
            nc.scalar.activation(
                squares[g][:],
                r_sb[g][:],
                ACT.Square,
                bias=r_sum[g][:, 0:1],
                scale=-float(C),
                accum_out=square_sums[g][:, 0:1],
            )
            nc.vector.tensor_scalar_mul(mean[g][:], r_sum[g][:], 1.0 / C)
            nc.scalar.activation(
                roots[g][:],
                square_sums[g][:],
                ACT.Sqrt,
                bias=tiny[:, 0:1],
                scale=1.0 / ((C - 1) * C * C),
                accum_out=std_eps[g][:],
            )

        def normalise(g):
            nc.vector.reciprocal(inv_std[g][:], std_eps[g][:])
            nc.vector.tensor_scalar(
                normed[g][:], r_sb[g][:], mean[g][:, 0:1], inv_std[g][:, 0:1], op0=ALU.subtract, op1=ALU.mult
            )

        def turn_back(g, bank):
            normed_ps = psum.tile([C, C], F32, name=f"normed_ps{g}", tag=bank)
            nc.tensor.transpose(normed_ps[:], normed[g][:], identity[:])
            return normed_ps

        def add_residual(g, normed_ps):
            for u in range(B):
                wrapped = max(SKEW - u - g * GROUP, 0)
                pieces = [(g * GROUP + wrapped + u - SKEW, wrapped, GROUP)]
                if wrapped:
                    pieces.append((T - wrapped, 0, wrapped))
                for position, begin, end in pieces:
                    nc.vector.scalar_tensor_tensor(
                        result[:, u, position : position + end - begin],
                        normed_ps[:, u * GROUP + begin : u * GROUP + end],
                        gamma_sb[:, 0:1],
                        shifted[:, u, position : position + end - begin],
                        op0=ALU.mult,
                        op1=ALU.add,
                    )

        warm_ps = psum.tile([C, WARM_LOOK_UPS * N], F32, name="warm_ps")

        def warm_by_look_ups(step):
            nc.tensor.matmul(
                warm_ps[:],
                w2_sb[:],
                unread[:, step + 1 - WARM_LOOK_UPS : step + 1, :, :].rearrange("c s u t -> c (s u t)"),
                start=True,
                stop=True,
            )

        def warm_by_group(g):
            for part in range(2 * WARM_LOOK_UPS * N // C):
                nc.tensor.matmul(warm_ps[:, :C], w2_sb[:], h_bf[g][:], start=True, stop=True)

        for ahead in range(T + LEAD):
            if ahead < T - 1:
                look_up(ahead, 0, B)
            elif ahead == T - 1:
                look_up(ahead, 0, B // 2)
                look_up(ahead, B // 2, B)
            if ahead == PE_TO:
                sum_on_tensor()
            step = ahead - LEAD
            if step >= PE_TO:
                sum_on_scalar(step)
            if step == SQRT_AT:
                nc.scalar.activation(warm[:], unread[:, step, 0, 0:1], ACT.Sqrt, bias=tiny[:, 0:1], scale=0.0)
            if WARM_FROM <= step < T - 1:
                warm_by_look_ups(step)
            if step == TAIL_FROM:
                round_tensor_sums()
                project_1(0)
            elif step == RELU_AT:
                project_2(0)
            elif step == STATISTICS_AT:
                statistics(0)

        project_1(1)
        nc.vector.tensor_tensor(
            shifted[:].rearrange("c u i -> c (u i)"),
            table[:].indirect(offsets[:]),
            beta_wide[:],
            ALU.add,
        )
        normalise(0)
        project_2(1)
        add_residual(0, turn_back(0, "h_ps1"))
        warm_by_group(1)
        statistics(1)
        normalise(1)
        add_residual(1, turn_back(1, "h_ps0"))
        nc.sync.dma_start(out, result[:].rearrange("c u i -> c (u i)"))
